import numpy as np
import ml_dtypes


def mxq(x, axis, fmt="e4m3"):
    dtype, down = {"e4m3": (ml_dtypes.float8_e4m3fn, 7), "e5m2": (ml_dtypes.float8_e5m2, 14)}[fmt]
    v = np.moveaxis(np.asarray(x, np.float32).astype(ml_dtypes.bfloat16).astype(np.float64), axis, -1)
    blocks = v.reshape(v.shape[:-1] + (-1, 32))
    amax = np.abs(blocks).max(-1, keepdims=True)
    byte = np.maximum(np.where(amax > 0, np.frexp(amax)[1] - 1 + 127, 0) - down, 1)
    scale = np.exp2(byte - 127.0)
    codes = (blocks / scale).astype(np.float32).astype(dtype).astype(np.float64)
    return np.moveaxis((codes * scale).reshape(v.shape), -1, axis)


WIDE = False


def mx_kscale(k):
    if not WIDE:
        return np.ones(k)
    levels = np.array([10, -10, 5, -5, 0])
    if k % 512:
        return np.exp2(np.random.permutation(np.resize(levels, k // 32))).repeat(32)
    a = np.empty((k // 512, 16))
    for p in range(k // 512):
        a[p, :8] = np.random.permutation(np.resize(levels, 8))
        for g in range(8):
            far = levels[np.abs(levels - a[p, g]) >= 10]
            a[p, g + 8] = far[np.random.randint(len(far))]
    return np.exp2(a.ravel()).repeat(32)


BF16 = ml_dtypes.bfloat16


def bf(x):
    return np.asarray(x, np.float32).astype(BF16)


def f64(x):
    return np.asarray(x).astype(np.float64)


N, IN_F, J, K = 256, 2048, 128, 16


def setup_inputs():
    s = mx_kscale(IN_F)
    s = s / s.max()
    return {"tensor": bf(np.random.standard_normal((N, IN_F)) * s),
            "T": bf(np.random.standard_normal((IN_F, J, K)) * 4.0 / (K * np.sqrt(IN_F)) / s[:, None, None])}


def core(tensor, T):
    x = f64(tensor).reshape(tensor.shape[0], -1)
    feats = (mxq(x, 1, "e4m3") @ mxq(f64(T).reshape(IN_F, J * K), 0, "e4m3")).reshape(N, J, K)
    diversity = np.stack([np.exp(-np.abs(feats[n][None, :, :] - feats).sum(axis=2)).sum(axis=0) for n in range(N)])
    return np.concatenate((x, diversity), axis=1)


def e4m3fn_bytes(y):
    return np.clip(np.asarray(y, np.float64), -448.0, 448.0).astype(np.float32).astype(ml_dtypes.float8_e4m3fn).view(np.uint8)


def reference(tensor, T):
    out = core(tensor, T)
    s = np.max(np.abs(out), axis=-1, keepdims=True) / 448.0
    return out, e4m3fn_bytes(out / s)

@@ -1,0 +1,396 @@
+from contextlib import ExitStack
+
+import concourse.mybir as mybir
+from concourse.masks import make_identity
+
+N_ROWS, IN_F, J, KD = 256, 2048, 128, 16
+FLOPS = 2 * N_ROWS * IN_F * J * KD + 3 * N_ROWS * N_ROWS * J * KD
+
+F32 = mybir.dt.float32
+BF16 = mybir.dt.bfloat16
+U32 = mybir.dt.uint32
+U8 = mybir.dt.uint8
+FP8X4 = mybir.dt.float8_e4m3fn_x4
+FP8 = mybir.dt.float8_e4m3fn
+ALU = mybir.AluOpType
+ACT = mybir.ActivationFunctionType
+AX = mybir.AxisListType
+
+P = 128
+S_MAX = 7
+V_N = 5
+W_MAX = KD - (S_MAX - 1) - V_N
+PLANES = KD + 1
+ONES_W = 16
+R = 4
+GROUPS = N_ROWS // R
+WIN = 128
+FXW = N_ROWS + WIN
+L_BANKS = 4
+FIRST_KICK = 8
+KICK_EVERY = 16
+KICK = 4
+CAST_SPLIT = 1440
+OUT_W = IN_F + J
+
+
+def tile_minibatchdiscriminator_kernel(tc, tensor, T, out_0, out_1):
+    nc = tc.nc
+    t_mat = T.rearrange("i j k -> i (j k)")
+    v_ks = list(range(KD - V_N, KD))
+
+    def scalar_planes(m):
+        return list(range(S_MAX - (m % 2)))
+
+    def own_planes(m):
+        first = [KD] if m % 2 == 1 else []
+        return first + list(range(S_MAX, KD - V_N))
+
+    with ExitStack() as ctx:
+        ctx.enter_context(tc.manual_schedule())
+        keep = ctx.enter_context(tc.tile_pool(name="keep", bufs=1))
+        psum = ctx.enter_context(tc.psum_pool(name="psum", bufs=1))
+
+        def bank(b, shape, name):
+            return psum.tile(shape, F32, name=name, tag="bank%d" % b)
+
+        ident = keep.tile([P, P], F32, name="ident", tag="ident")
+        make_identity(nc, ident[:])
+        zeros = keep.tile([P, P], F32, name="zeros", tag="zeros")
+        nc.vector.memset(zeros[:], 0.0)
+        ones = keep.tile([P, ONES_W], F32, name="ones", tag="ones")
+        nc.vector.memset(ones[:], 1.0)
+        warm = keep.tile([P, 1], F32, name="warm", tag="warm")
+        nc.scalar.activation(out=warm[:], in_=zeros[:, 0:1], func=ACT.Exp)
+
+        xb = []
+        for i in range(2):
+            xbi = keep.tile([P, IN_F], BF16, name="xb%d" % i, tag="xb%d" % i)
+            nc.sync.dma_start(out=xbi[:], in_=tensor[i * P : (i + 1) * P, :])
+            xb.append(xbi)
+        o32 = []
+        for i in range(2):
+            o32i = keep.tile([P, OUT_W], F32, name="o32_%d" % i, tag="o32_%d" % i)
+            o32.append(o32i)
+        fsb = []
+        for i in range(2):
+            fsbi = keep.tile([P, KD, J], F32, name="fsb%d" % i, tag="fsb%d" % i)
+            fsb.append(fsbi)
+        fx = keep.tile([P, PLANES, FXW], F32, name="fx", tag="fx")
+        hns = []
+        for par in range(2):
+            hnp = keep.tile([P, FXW], F32, name="hn%d" % par, tag="hn%d" % par)
+            hns.append(hnp)
+        maskb = keep.tile([P, 1], F32, name="maskb", tag="maskb")
+        xmax = keep.tile([P, 2], F32, name="xmax", tag="xmax")
+        xq = keep.tile([P, 4 * N_ROWS], U32, name="xq", tag="xq", align_bytes=64)
+        xs = keep.tile([P, 4 * N_ROWS], U8, name="xs", tag="xs", align_bytes=64)
+
+        fb = {}
+        with tc.tile_pool(name="ph1", bufs=1) as ph1:
+            raws = []
+            for q in range(8):
+                c, h = divmod(q, 2)
+                raw = ph1.tile([P, 4, 1024], BF16, name="raw", tag="raw", bufs=8)
+                nc.sync.dma_start(
+                    out=raw[:],
+                    in_=t_mat[512 * c : 512 * (c + 1), 1024 * h : 1024 * (h + 1)].rearrange("(p t) w -> p t w", t=4),
+                )
+                raws.append(raw)
+
+            xg = ph1.tile([P, 4 * N_ROWS * 4], BF16, name="xg", tag="xg", align_bytes=64)
+            tq = ph1.tile([P, 4, IN_F], U32, name="tq", tag="tq", align_bytes=64)
+            ts = ph1.tile([P, 4, IN_F], U8, name="ts", tag="ts", align_bytes=64)
+
+            xg_words = xg[:].bitcast(F32).rearrange("p (g n u) -> p g n u", g=4, u=2)
+            for gp in range(2):
+                for i in range(2):
+                    words = xb[i][:].bitcast(F32)
+                    xt = bank(2 * gp + i, [P, 2, 2, P], "xt")
+                    for gg in range(2):
+                        g = 2 * gp + gg
+                        for u in range(2):
+                            nc.tensor.transpose(xt[:, gg, u, :], words[:, 256 * g + u : 256 * (g + 1) : 2], ident[:])
+                    dst = xg_words[:, 2 * gp : 2 * gp + 2, i * P : (i + 1) * P, :]
+                    src = xt[:].rearrange("p g u r -> p g r u")
+                    if i == 0:
+                        nc.vector.tensor_copy(out=dst, in_=src)
+                    else:
+                        nc.scalar.copy(out=dst, in_=src)
+            for gp in range(2):
+                nc.vector.quantize_mx(
+                    out=xq[:, 512 * gp : 512 * (gp + 1)].bitcast(FP8X4),
+                    scales=xs[:, 512 * gp : 512 * (gp + 1)],
+                    in_=xg[:, 2048 * gp : 2048 * (gp + 1)],
+                )
+
+            for i in range(2):
+                for wq in range(4):
+                    fb[(i, wq)] = bank(4 * i + wq, [P, 512], "fb")
+
+            tgs = {}
+
+            def interleave(q):
+                tg = ph1.tile([P, 1024, 4], BF16, name="tg", tag="tg", bufs=3, align_bytes=64)
+                tgs[q] = tg
+                raw = raws[q]
+                nc.vector.tensor_copy(out=tg[:, 0:512, :], in_=raw[:, :, 0:512].rearrange("p t w -> p w t"))
+                nc.scalar.copy(out=tg[:, 512:1024, :], in_=raw[:, :, 512:1024].rearrange("p t w -> p w t"))
+
+            def quantise_and_multiply(q):
+                c, h = divmod(q, 2)
+                cols = slice(1024 * h, 1024 * (h + 1))
+                nc.vector.quantize_mx(
+                    out=tq[:, c, cols].bitcast(FP8X4),
+                    scales=ts[:, c, cols],
+                    in_=tgs[q][:].rearrange("p w t -> p (w t)"),
+                )
+                for wq in (2 * h, 2 * h + 1):
+                    for i in range(2):
+                        n_cols = slice(256 * c + P * i, 256 * c + P * (i + 1))
+                        w_cols = slice(512 * wq, 512 * (wq + 1))
+                        nc.tensor.matmul_mx(
+                            out=fb[(i, wq)][:],
+                            lhsT=xq[:, n_cols].bitcast(FP8X4),
+                            lhsT_scale=xs[:, n_cols],
+                            rhs=tq[:, c, w_cols].bitcast(FP8X4),
+                            rhs_scale=ts[:, c, w_cols],
+                            start=(c == 0),
+                            stop=(c == 3),
+                        )
+
+            for q in range(9):
+                if q < 8:
+                    interleave(q)
+                if q >= 1:
+                    quantise_and_multiply(q - 1)
+
+        for i in range(2):
+            for wq in range(4):
+                dst = fsb[i][:, :, 32 * wq : 32 * (wq + 1)]
+                src = fb[(i, wq)][:].rearrange("p (j k) -> p k j", k=KD)
+                if wq % 2 == 0:
+                    nc.vector.tensor_copy(out=dst, in_=src)
+                else:
+                    nc.scalar.copy(out=dst, in_=src)
+
+        for kp in range(8):
+            pk = bank(kp, [P, 2, N_ROWS], "pk")
+            for kk in range(2):
+                for i in range(2):
+                    nc.tensor.transpose(pk[:, kk, i * P : (i + 1) * P], fsb[i][:, 2 * kp + kk, :], ident[:])
+            for kk in range(2):
+                k = 2 * kp + kk
+                if k < S_MAX:
+                    nc.scalar.activation(out=fx[:, k, 0:N_ROWS], in_=pk[:, kk, :], func=ACT.Copy, scale=0.5)
+                if k >= S_MAX - 1:
+                    plane = KD if k == S_MAX - 1 else k
+                    nc.vector.tensor_copy(out=fx[:, plane, 0:N_ROWS], in_=pk[:, kk, :])
+
+        hp = bank(0, [P, N_ROWS], "hp")
+        vec_ks = list(range(S_MAX, KD))
+        for i in range(2):
+            for idx, k in enumerate(vec_ks):
+                nc.tensor.matmul(
+                    out=hp[:, i * P : (i + 1) * P],
+                    lhsT=fsb[i][:, k, :],
+                    rhs=ident[:],
+                    is_transpose=True,
+                    start=(idx == 0),
+                    stop=(idx == len(vec_ks) - 1),
+                )
+        nc.vector.tensor_scalar(out=hns[0][:, 0:N_ROWS], in0=hp[:], scalar1=-0.5, scalar2=None, op0=ALU.mult)
+        nc.vector.tensor_tensor(out=hns[1][:, 0:N_ROWS], in0=hns[0][:, 0:N_ROWS], in1=fx[:, S_MAX - 1, 0:N_ROWS], op=ALU.subtract)
+        nc.vector.tensor_scalar(out=maskb[:], in0=ident[:, P - 1 : P], scalar1=-30000.0, scalar2=None, op0=ALU.mult)
+
+        rb = bank(5, [P, N_ROWS + ONES_W], "rb")
+        c_even = bank(6, [P, FXW], "c_even")
+        c_odd = bank(7, [P, FXW], "c_odd")
+        for cb in (c_even, c_odd):
+            for z in range(3):
+                nc.tensor.matmul(
+                    out=cb[:, z * P : (z + 1) * P], lhsT=zeros[:], rhs=ident[:], is_transpose=True, start=(z == 0), stop=False
+                )
+
+        scratch = bank(4, [P, 512], "scratch")
+
+        def kick(passes):
+            for rep in range(passes):
+                nc.tensor.matmul_mx(
+                    out=scratch[:],
+                    lhsT=xq[:, 0:P].bitcast(FP8X4),
+                    lhsT_scale=xs[:, 0:P],
+                    rhs=xq[:, 0:512].bitcast(FP8X4),
+                    rhs_scale=xs[:, 0:512],
+                    start=True,
+                    stop=True,
+                )
+
+        kick(FIRST_KICK)
+
+        sap = ctx.enter_context(tc.tile_pool(name="sap", bufs=3))
+        vap = ctx.enter_context(tc.tile_pool(name="vap", bufs=3))
+        epl = ctx.enter_context(tc.tile_pool(name="epl", bufs=3))
+        fin = ctx.enter_context(tc.tile_pool(name="fin", bufs=1))
+        sas, vas, lbs, ets = {}, {}, {}, {}
+
+        def produce(g):
+            sa = sap.tile([P, R, S_MAX, WIN], F32, name="sa", tag="sa")
+            va = vap.tile([P, R, W_MAX + 1, WIN], F32, name="va", tag="va")
+            sas[g] = sa
+            vas[g] = va
+            for r in range(R):
+                m = R * g + r
+                for idx, k in enumerate(scalar_planes(m)):
+                    nc.scalar.activation(
+                        out=sa[:, r, idx, :], in_=fx[:, k, m + 1 : m + 1 + WIN], func=ACT.Abs, scale=-1.0, bias=fx[:, k, m : m + 1]
+                    )
+
+            def own_tile(r, idx):
+                m = R * g + r
+                k = own_planes(m)[idx]
+                if idx == 0:
+                    nc.vector.tensor_scalar(
+                        out=va[:, r, idx, :],
+                        in0=fx[:, k, m + 1 : m + 1 + WIN],
+                        scalar1=fx[:, k, m : m + 1],
+                        scalar2=hns[m % 2][:, m : m + 1],
+                        op0=ALU.max,
+                        op1=ALU.add,
+                    )
+                else:
+                    nc.vector.tensor_scalar(
+                        out=va[:, r, idx, :],
+                        in0=fx[:, k, m + 1 : m + 1 + WIN],
+                        scalar1=fx[:, k, m : m + 1],
+                        scalar2=None,
+                        op0=ALU.max,
+                    )
+
+            def chain_link(r, idx):
+                m = R * g + r
+                k = v_ks[idx]
+                nc.vector.scalar_tensor_tensor(
+                    out=va[:, r, W_MAX, :],
+                    in0=fx[:, k, m + 1 : m + 1 + WIN],
+                    scalar=fx[:, k, m : m + 1],
+                    in1=(hns[m % 2][:, m + 1 : m + 1 + WIN] if idx == 0 else va[:, r, W_MAX, :]),
+                    op0=ALU.max,
+                    op1=ALU.add,
+                )
+
+            for pair in range(R // 2):
+                pair_rows = (2 * pair, 2 * pair + 1)
+                own = []
+                for idx in range(W_MAX):
+                    for r in pair_rows:
+                        if idx < len(own_planes(R * g + r)):
+                            own.append((r, idx))
+                for idx in range(V_N):
+                    for r in pair_rows:
+                        chain_link(r, idx)
+                    lo = (idx * len(own)) // V_N
+                    hi = ((idx + 1) * len(own)) // V_N
+                    for r, widx in own[lo:hi]:
+                        own_tile(r, widx)
+
+        def accumulate_row(g, r):
+            if r == 0:
+                lbs[g] = bank(g % L_BANKS, [P, R, J], "lb")
+            lb = lbs[g]
+            m = R * g + r
+            srcs = [vas[g][:, r, idx, :] for idx in range(len(own_planes(m)))]
+            srcs.extend([sas[g][:, r, idx, :] for idx in range(len(scalar_planes(m)))])
+            srcs.append(vas[g][:, r, W_MAX, :])
+            for idx, src in enumerate(srcs):
+                nc.tensor.matmul(
+                    out=lb[:, r, :], lhsT=src, rhs=ident[:], is_transpose=True, start=(idx == 0), stop=(idx == len(srcs) - 1)
+                )
+
+        def expo(g):
+            et = epl.tile([P, R, J], F32, name="et", tag="et")
+            ets[g] = et
+            bias = maskb[:, 0:1] if R * g >= WIN else zeros[:, 0:1]
+            nc.scalar.activation(out=et[:], in_=lbs[g][:], func=ACT.Exp, scale=-2.0, bias=bias)
+
+        def fold_row(g, r):
+            m = R * g + r
+            if m % 2 == 1:
+                dst = c_even[:, m + 1 : m + 1 + WIN]
+            else:
+                dst = c_odd[:, m : m + WIN]
+            nc.tensor.matmul(out=dst, lhsT=ets[g][:, r, :], rhs=ident[:], is_transpose=True, start=False, stop=(m >= N_ROWS - 2))
+            nc.tensor.matmul(out=rb[:, m : m + ONES_W], lhsT=ets[g][:, r, :], rhs=ones[:], start=True, stop=True)
+
+        for it in range(GROUPS + 3):
+            if 8 <= it < 8 + PLANES:
+                nc.vector.tensor_copy(out=fx[:, it - 8, N_ROWS:FXW], in_=fx[:, it - 8, 0:WIN])
+            if 8 + PLANES <= it < 10 + PLANES:
+                hnp = hns[it - 8 - PLANES]
+                nc.vector.tensor_copy(out=hnp[:, N_ROWS:FXW], in_=hnp[:, 0:WIN])
+            if it < GROUPS:
+                produce(it)
+            if it == GROUPS:
+                nc.vector.tensor_copy(out=o32[1][:, 0:IN_F], in_=xb[1][:])
+                nc.sync.dma_start(out=out_0[P : 2 * P, 0:IN_F], in_=o32[1][:, 0:IN_F])
+                for i in range(2):
+                    nc.vector.tensor_reduce(
+                        out=xmax[:, i : i + 1], in_=xb[i][:], axis=AX.X, op=ALU.max, apply_absolute_value=True
+                    )
+            if it >= KICK_EVERY and it % KICK_EVERY == 0 and it < GROUPS:
+                kick(KICK)
+            for r in range(R):
+                if 0 <= it - 1 < GROUPS:
+                    accumulate_row(it - 1, r)
+                if 0 <= it - 3 < GROUPS:
+                    fold_row(it - 3, r)
+            if 0 <= it - 2 < GROUPS:
+                expo(it - 2)
+            if it == GROUPS:
+                nc.scalar.copy(out=o32[0][:, 0:IN_F], in_=xb[0][:])
+                nc.sync.dma_start(out=out_0[0:P, 0:IN_F], in_=o32[0][:, 0:IN_F])
+
+        dv = fin.tile([P, N_ROWS], F32, name="dv", tag="dv")
+        nc.vector.tensor_scalar(out=dv[:], in0=rb[:, 0:N_ROWS], scalar1=1.0, scalar2=None, op0=ALU.add)
+        nc.vector.tensor_tensor(out=dv[:], in0=c_even[:, 0:N_ROWS], in1=dv[:], op=ALU.add)
+        nc.vector.tensor_tensor(out=dv[:, 0:WIN], in0=c_even[:, N_ROWS:FXW], in1=dv[:, 0:WIN], op=ALU.add)
+        nc.vector.tensor_tensor(out=dv[:, 1:N_ROWS], in0=c_odd[:, 0 : N_ROWS - 1], in1=dv[:, 1:N_ROWS], op=ALU.add)
+        nc.vector.tensor_tensor(out=dv[:, 0:WIN], in0=c_odd[:, N_ROWS - 1 : FXW - 1], in1=dv[:, 0:WIN], op=ALU.add)
+        dt_ps = bank(0, [P, 2, J], "dt_ps")
+        dmax = fin.tile([P, 2], F32, name="dmax", tag="dmax")
+        for i in range(2):
+            nc.tensor.transpose(dt_ps[:, i, :], dv[:, i * P : (i + 1) * P], ident[:])
+        for i in range(2):
+            nc.vector.tensor_scalar(
+                out=o32[i][:, IN_F:OUT_W],
+                in0=dt_ps[:, i, :],
+                scalar1=1.0,
+                scalar2=None,
+                op0=ALU.mult,
+                op1=ALU.max,
+                accum_out=dmax[:, i : i + 1],
+            )
+            nc.sync.dma_start(out=out_0[i * P : (i + 1) * P, IN_F:OUT_W], in_=o32[i][:, IN_F:OUT_W])
+        amax = fin.tile([P, 2], F32, name="amax", tag="amax")
+        nc.vector.tensor_tensor(out=amax[:], in0=dmax[:], in1=xmax[:], op=ALU.max)
+        rcp = fin.tile([P, 2], F32, name="rcp", tag="rcp")
+        nc.vector.reciprocal(out=rcp[:], in_=amax[:])
+        fac = fin.tile([P, 2], F32, name="fac", tag="fac")
+        nc.vector.tensor_scalar(out=fac[:], in0=rcp[:], scalar1=448.0, scalar2=None, op0=ALU.mult)
+        for i in range(2):
+            rows = slice(i * P, (i + 1) * P)
+            o8v = fin.tile([P, CAST_SPLIT], FP8, name="o8v%d" % i, tag="o8v%d" % i)
+            o8s = fin.tile([P, OUT_W - CAST_SPLIT], FP8, name="o8s%d" % i, tag="o8s%d" % i)
+            nc.vector.tensor_scalar(
+                out=o8v[:], in0=o32[i][:, 0:CAST_SPLIT], scalar1=fac[:, i : i + 1], scalar2=None, op0=ALU.mult, saturate=False
+            )
+            nc.scalar.activation(
+                out=o8s[:],
+                in_=o32[i][:, CAST_SPLIT:OUT_W],
+                func=ACT.Identity,
+                scale=fac[:, i : i + 1],
+                bias=zeros[:, 0:1],
+                saturate=False,
+            )
+            nc.sync.dma_start(out=out_1[rows, 0:CAST_SPLIT], in_=o8v[:].bitcast(U8))
+            nc.sync.dma_start(out=out_1[rows, CAST_SPLIT:OUT_W], in_=o8s[:].bitcast(U8))

@@ -279,29 +279,27 @@ def tile_minibatchdiscriminator_kernel(tc, tensor, T, out_0, out_1):
                     op1=ALU.add,
                 )
 
-            for pair in range(R // 2):
-                pair_rows = (2 * pair, 2 * pair + 1)
-                own = []
-                for idx in range(W_MAX):
-                    for r in pair_rows:
-                        if idx < len(own_planes(R * g + r)):
-                            own.append((r, idx))
-                for idx in range(V_N):
-                    for r in pair_rows:
-                        chain_link(r, idx)
-                    lo = (idx * len(own)) // V_N
-                    hi = ((idx + 1) * len(own)) // V_N
-                    for r, widx in own[lo:hi]:
-                        own_tile(r, widx)
+            own = []
+            for idx in range(W_MAX):
+                for r in range(R):
+                    if idx < len(own_planes(R * g + r)):
+                        own.append((r, idx))
+            for idx in range(V_N):
+                for r in range(R):
+                    chain_link(r, idx)
+                lo = (idx * len(own)) // (V_N - 1)
+                hi = ((idx + 1) * len(own)) // (V_N - 1)
+                for r, widx in own[lo:hi]:
+                    own_tile(r, widx)
 
         def accumulate_row(g, r):
             if r == 0:
                 lbs[g] = bank(g % L_BANKS, [P, R, J], "lb")
             lb = lbs[g]
             m = R * g + r
-            srcs = [vas[g][:, r, idx, :] for idx in range(len(own_planes(m)))]
+            srcs = [vas[g][:, r, W_MAX, :]]
+            srcs.extend([vas[g][:, r, idx, :] for idx in range(len(own_planes(m)))])
             srcs.extend([sas[g][:, r, idx, :] for idx in range(len(scalar_planes(m)))])
-            srcs.append(vas[g][:, r, W_MAX, :])
             for idx, src in enumerate(srcs):
                 nc.tensor.matmul(
                     out=lb[:, r, :], lhsT=src, rhs=ident[:], is_transpose=True, start=(idx == 0), stop=(idx == len(srcs) - 1)

@@ -27,7 +27,7 @@ GROUPS = N_ROWS // R
 WIN = 128
 FXW = N_ROWS + WIN
 L_BANKS = 4
-FIRST_KICK = 8
+FIRST_KICK = 15
 KICK_EVERY = 16
 KICK = 4
 CAST_SPLIT = 1440

@@ -17,12 +17,13 @@ ACT = mybir.ActivationFunctionType
 AX = mybir.AxisListType
 
 P = 128
-S_MAX = 7
-V_N = 5
-W_MAX = KD - (S_MAX - 1) - V_N
+R = 4
+S_ROW = (7, 7, 7, 6)
+CHAIN_ROW = (5, 6, 5, 6)
+S_MAX = max(S_ROW)
+W_MAX = max([KD - S_ROW[r] - CHAIN_ROW[r] for r in range(R)])
 PLANES = KD + 1
 ONES_W = 16
-R = 4
 GROUPS = N_ROWS // R
 WIN = 128
 FXW = N_ROWS + WIN
@@ -37,14 +38,21 @@ OUT_W = IN_F + J
 def tile_minibatchdiscriminator_kernel(tc, tensor, T, out_0, out_1):
     nc = tc.nc
     t_mat = T.rearrange("i j k -> i (j k)")
-    v_ks = list(range(KD - V_N, KD))
 
     def scalar_planes(m):
-        return list(range(S_MAX - (m % 2)))
+        return list(range(S_ROW[m % R]))
+
+    def vector_planes(m):
+        return [KD if k == S_MAX - 1 else k for k in range(S_ROW[m % R], KD)]
 
     def own_planes(m):
-        first = [KD] if m % 2 == 1 else []
-        return first + list(range(S_MAX, KD - V_N))
+        return vector_planes(m)[: KD - S_ROW[m % R] - CHAIN_ROW[m % R]]
+
+    def chain_planes(m):
+        return vector_planes(m)[KD - S_ROW[m % R] - CHAIN_ROW[m % R] :]
+
+    def hn_of(m):
+        return hns[S_MAX - S_ROW[m % R]]
 
     with ExitStack() as ctx:
         ctx.enter_context(tc.manual_schedule())
@@ -254,7 +262,7 @@ def tile_minibatchdiscriminator_kernel(tc, tensor, T, out_0, out_1):
                         out=va[:, r, idx, :],
                         in0=fx[:, k, m + 1 : m + 1 + WIN],
                         scalar1=fx[:, k, m : m + 1],
-                        scalar2=hns[m % 2][:, m : m + 1],
+                        scalar2=hn_of(m)[:, m : m + 1],
                         op0=ALU.max,
                         op1=ALU.add,
                     )
@@ -269,12 +277,12 @@ def tile_minibatchdiscriminator_kernel(tc, tensor, T, out_0, out_1):
 
             def chain_link(r, idx):
                 m = R * g + r
-                k = v_ks[idx]
+                k = chain_planes(m)[idx]
                 nc.vector.scalar_tensor_tensor(
                     out=va[:, r, W_MAX, :],
                     in0=fx[:, k, m + 1 : m + 1 + WIN],
                     scalar=fx[:, k, m : m + 1],
-                    in1=(hns[m % 2][:, m + 1 : m + 1 + WIN] if idx == 0 else va[:, r, W_MAX, :]),
+                    in1=(hn_of(m)[:, m + 1 : m + 1 + WIN] if idx == 0 else va[:, r, W_MAX, :]),
                     op0=ALU.max,
                     op1=ALU.add,
                 )
@@ -284,11 +292,14 @@ def tile_minibatchdiscriminator_kernel(tc, tensor, T, out_0, out_1):
                 for r in range(R):
                     if idx < len(own_planes(R * g + r)):
                         own.append((r, idx))
-            for idx in range(V_N):
+            steps = max(CHAIN_ROW)
+            for step in range(steps):
                 for r in range(R):
-                    chain_link(r, idx)
-                lo = (idx * len(own)) // (V_N - 1)
-                hi = ((idx + 1) * len(own)) // (V_N - 1)
+                    idx = step - (steps - CHAIN_ROW[r])
+                    if idx >= 0:
+                        chain_link(r, idx)
+                lo = -((-step * len(own)) // (steps - 1))
+                hi = -((-(step + 1) * len(own)) // (steps - 1))
                 for r, widx in own[lo:hi]:
                     own_tile(r, widx)
 

@@ -22,13 +22,17 @@ S_ROW = (7, 7, 7, 6)
 CHAIN_ROW = (5, 6, 5, 6)
 S_MAX = max(S_ROW)
 W_MAX = max([KD - S_ROW[r] - CHAIN_ROW[r] for r in range(R)])
+C_MAX = max(CHAIN_ROW)
+OWN_AHEAD = 1
+FIRST_ROWS = 2
+FIRST_AHEAD = C_MAX - 2
 PLANES = KD + 1
-ONES_W = 16
+ONES_W = 24
 GROUPS = N_ROWS // R
 WIN = 128
 FXW = N_ROWS + WIN
 L_BANKS = 4
-FIRST_KICK = 15
+FIRST_KICK = 8
 KICK_EVERY = 16
 KICK = 4
 CAST_SPLIT = 1440
@@ -237,80 +241,80 @@ def tile_minibatchdiscriminator_kernel(tc, tensor, T, out_0, out_1):
         kick(FIRST_KICK)
 
         sap = ctx.enter_context(tc.tile_pool(name="sap", bufs=3))
-        vap = ctx.enter_context(tc.tile_pool(name="vap", bufs=3))
+        vap = ctx.enter_context(tc.tile_pool(name="vap", bufs=4))
         epl = ctx.enter_context(tc.tile_pool(name="epl", bufs=3))
         fin = ctx.enter_context(tc.tile_pool(name="fin", bufs=1))
         sas, vas, lbs, ets = {}, {}, {}, {}
 
-        def produce(g):
-            sa = sap.tile([P, R, S_MAX, WIN], F32, name="sa", tag="sa")
-            va = vap.tile([P, R, W_MAX + 1, WIN], F32, name="va", tag="va")
-            sas[g] = sa
-            vas[g] = va
-            for r in range(R):
-                m = R * g + r
-                for idx, k in enumerate(scalar_planes(m)):
-                    nc.scalar.activation(
-                        out=sa[:, r, idx, :], in_=fx[:, k, m + 1 : m + 1 + WIN], func=ACT.Abs, scale=-1.0, bias=fx[:, k, m : m + 1]
-                    )
+        def scalar_row(m):
+            g, r = divmod(m, R)
+            if r == 0:
+                sa = sap.tile([P, R, S_MAX, WIN], F32, name="sa", tag="sa")
+                sas[g] = sa
+            for idx, k in enumerate(scalar_planes(m)):
+                nc.scalar.activation(
+                    out=sas[g][:, r, idx, :], in_=fx[:, k, m + 1 : m + 1 + WIN], func=ACT.Abs, scale=-1.0, bias=fx[:, k, m : m + 1]
+                )
 
-            def own_tile(r, idx):
-                m = R * g + r
-                k = own_planes(m)[idx]
-                if idx == 0:
-                    nc.vector.tensor_scalar(
-                        out=va[:, r, idx, :],
-                        in0=fx[:, k, m + 1 : m + 1 + WIN],
-                        scalar1=fx[:, k, m : m + 1],
-                        scalar2=hn_of(m)[:, m : m + 1],
-                        op0=ALU.max,
-                        op1=ALU.add,
-                    )
-                else:
-                    nc.vector.tensor_scalar(
-                        out=va[:, r, idx, :],
-                        in0=fx[:, k, m + 1 : m + 1 + WIN],
-                        scalar1=fx[:, k, m : m + 1],
-                        scalar2=None,
-                        op0=ALU.max,
-                    )
+        def vector_tiles(m):
+            g = m // R
+            if g not in vas:
+                va = vap.tile([P, R, W_MAX + 1, WIN], F32, name="va", tag="va")
+                vas[g] = va
+            return vas[g]
 
-            def chain_link(r, idx):
-                m = R * g + r
-                k = chain_planes(m)[idx]
-                nc.vector.scalar_tensor_tensor(
-                    out=va[:, r, W_MAX, :],
+        def own_tile(m, idx):
+            va = vector_tiles(m)
+            k = own_planes(m)[idx]
+            if idx == 0:
+                nc.vector.tensor_scalar(
+                    out=va[:, m % R, idx, :],
                     in0=fx[:, k, m + 1 : m + 1 + WIN],
-                    scalar=fx[:, k, m : m + 1],
-                    in1=(hn_of(m)[:, m + 1 : m + 1 + WIN] if idx == 0 else va[:, r, W_MAX, :]),
+                    scalar1=fx[:, k, m : m + 1],
+                    scalar2=hn_of(m)[:, m : m + 1],
                     op0=ALU.max,
                     op1=ALU.add,
                 )
+            else:
+                nc.vector.tensor_scalar(
+                    out=va[:, m % R, idx, :],
+                    in0=fx[:, k, m + 1 : m + 1 + WIN],
+                    scalar1=fx[:, k, m : m + 1],
+                    scalar2=None,
+                    op0=ALU.max,
+                )
 
-            own = []
-            for idx in range(W_MAX):
-                for r in range(R):
-                    if idx < len(own_planes(R * g + r)):
-                        own.append((r, idx))
-            steps = max(CHAIN_ROW)
-            for step in range(steps):
-                for r in range(R):
-                    idx = step - (steps - CHAIN_ROW[r])
-                    if idx >= 0:
-                        chain_link(r, idx)
-                lo = -((-step * len(own)) // (steps - 1))
-                hi = -((-(step + 1) * len(own)) // (steps - 1))
-                for r, widx in own[lo:hi]:
-                    own_tile(r, widx)
+        def chain_link(m, idx):
+            va = vector_tiles(m)
+            k = chain_planes(m)[idx]
+            nc.vector.scalar_tensor_tensor(
+                out=va[:, m % R, W_MAX, :],
+                in0=fx[:, k, m + 1 : m + 1 + WIN],
+                scalar=fx[:, k, m : m + 1],
+                in1=(hn_of(m)[:, m + 1 : m + 1 + WIN] if idx == 0 else va[:, m % R, W_MAX, :]),
+                op0=ALU.max,
+                op1=ALU.add,
+            )
 
-        def accumulate_row(g, r):
+        def vector_slot(t):
+            for d in range(C_MAX):
+                m = t + d
+                if 0 <= m < N_ROWS and CHAIN_ROW[m % R] - 1 - d >= 0:
+                    chain_link(m, CHAIN_ROW[m % R] - 1 - d)
+            for ahead in (OWN_AHEAD, FIRST_AHEAD):
+                m = t + ahead
+                if 0 <= m < N_ROWS and (m < FIRST_ROWS) == (ahead == FIRST_AHEAD):
+                    for idx in range(len(own_planes(m))):
+                        own_tile(m, idx)
+
+        def accumulate_row(m):
+            g, r = divmod(m, R)
             if r == 0:
                 lbs[g] = bank(g % L_BANKS, [P, R, J], "lb")
             lb = lbs[g]
-            m = R * g + r
-            srcs = [vas[g][:, r, W_MAX, :]]
+            srcs = [sas[g][:, r, idx, :] for idx in range(len(scalar_planes(m)))]
             srcs.extend([vas[g][:, r, idx, :] for idx in range(len(own_planes(m)))])
-            srcs.extend([sas[g][:, r, idx, :] for idx in range(len(scalar_planes(m)))])
+            srcs.append(vas[g][:, r, W_MAX, :])
             for idx, src in enumerate(srcs):
                 nc.tensor.matmul(
                     out=lb[:, r, :], lhsT=src, rhs=ident[:], is_transpose=True, start=(idx == 0), stop=(idx == len(srcs) - 1)
@@ -322,8 +326,8 @@ def tile_minibatchdiscriminator_kernel(tc, tensor, T, out_0, out_1):
             bias = maskb[:, 0:1] if R * g >= WIN else zeros[:, 0:1]
             nc.scalar.activation(out=et[:], in_=lbs[g][:], func=ACT.Exp, scale=-2.0, bias=bias)
 
-        def fold_row(g, r):
-            m = R * g + r
+        def fold_row(m):
+            g, r = divmod(m, R)
             if m % 2 == 1:
                 dst = c_even[:, m + 1 : m + 1 + WIN]
             else:
@@ -331,31 +335,31 @@ def tile_minibatchdiscriminator_kernel(tc, tensor, T, out_0, out_1):
             nc.tensor.matmul(out=dst, lhsT=ets[g][:, r, :], rhs=ident[:], is_transpose=True, start=False, stop=(m >= N_ROWS - 2))
             nc.tensor.matmul(out=rb[:, m : m + ONES_W], lhsT=ets[g][:, r, :], rhs=ones[:], start=True, stop=True)
 
-        for it in range(GROUPS + 3):
-            if 8 <= it < 8 + PLANES:
-                nc.vector.tensor_copy(out=fx[:, it - 8, N_ROWS:FXW], in_=fx[:, it - 8, 0:WIN])
-            if 8 + PLANES <= it < 10 + PLANES:
-                hnp = hns[it - 8 - PLANES]
+        for t in range(-C_MAX, N_ROWS + 2 * R):
+            if 0 <= t + R < N_ROWS:
+                scalar_row(t + R)
+            if t % R == 0 and 8 <= t // R < 8 + PLANES:
+                nc.vector.tensor_copy(out=fx[:, t // R - 8, N_ROWS:FXW], in_=fx[:, t // R - 8, 0:WIN])
+            if t % R == 0 and 8 + PLANES <= t // R < 10 + PLANES:
+                hnp = hns[t // R - 8 - PLANES]
                 nc.vector.tensor_copy(out=hnp[:, N_ROWS:FXW], in_=hnp[:, 0:WIN])
-            if it < GROUPS:
-                produce(it)
-            if it == GROUPS:
+            vector_slot(t)
+            if t == N_ROWS:
                 nc.vector.tensor_copy(out=o32[1][:, 0:IN_F], in_=xb[1][:])
                 nc.sync.dma_start(out=out_0[P : 2 * P, 0:IN_F], in_=o32[1][:, 0:IN_F])
                 for i in range(2):
                     nc.vector.tensor_reduce(
                         out=xmax[:, i : i + 1], in_=xb[i][:], axis=AX.X, op=ALU.max, apply_absolute_value=True
                     )
-            if it >= KICK_EVERY and it % KICK_EVERY == 0 and it < GROUPS:
+            if 0 < t < N_ROWS - R and (t + R) % (R * KICK_EVERY) == 0:
                 kick(KICK)
-            for r in range(R):
-                if 0 <= it - 1 < GROUPS:
-                    accumulate_row(it - 1, r)
-                if 0 <= it - 3 < GROUPS:
-                    fold_row(it - 3, r)
-            if 0 <= it - 2 < GROUPS:
-                expo(it - 2)
-            if it == GROUPS:
+            if 0 <= t < N_ROWS:
+                accumulate_row(t)
+            if 0 <= t - 2 * R < N_ROWS:
+                fold_row(t - 2 * R)
+            if t % R == R - 1 and 0 <= t // R - 1 < GROUPS:
+                expo(t // R - 1)
+            if t == N_ROWS - 1:
                 nc.scalar.copy(out=o32[0][:, 0:IN_F], in_=xb[0][:])
                 nc.sync.dma_start(out=out_0[0:P, 0:IN_F], in_=o32[0][:, 0:IN_F])
 

@@ -35,6 +35,7 @@ L_BANKS = 4
 FIRST_KICK = 8
 KICK_EVERY = 16
 KICK = 4
+IDLE_TURNS = 3
 CAST_SPLIT = 1440
 OUT_W = IN_F + J
 
@@ -355,6 +356,9 @@ def tile_minibatchdiscriminator_kernel(tc, tensor, T, out_0, out_1):
                 kick(KICK)
             if 0 <= t < N_ROWS:
                 accumulate_row(t)
+            if 0 <= t < 2 * R:
+                for rep in range(IDLE_TURNS):
+                    nc.tensor.transpose(scratch[:, 0:P], ident[:], ident[:])
             if 0 <= t - 2 * R < N_ROWS:
                 fold_row(t - 2 * R)
             if t % R == R - 1 and 0 <= t // R - 1 < GROUPS:

@@ -32,7 +32,9 @@ GROUPS = N_ROWS // R
 WIN = 128
 FXW = N_ROWS + WIN
 L_BANKS = 4
-FIRST_KICK = 8
+TURN_ORDER = (5, 4, 3, 6, 7, 0, 1, 2)
+V_COPIES = (8, 9, 10, 11)
+FIRST_KICK = 4
 KICK_EVERY = 16
 KICK = 4
 IDLE_TURNS = 3
@@ -75,6 +77,8 @@ def tile_minibatchdiscriminator_kernel(tc, tensor, T, out_0, out_1):
         nc.vector.memset(ones[:], 1.0)
         warm = keep.tile([P, 1], F32, name="warm", tag="warm")
         nc.scalar.activation(out=warm[:], in_=zeros[:, 0:1], func=ACT.Exp)
+        maskb = keep.tile([P, 1], F32, name="maskb", tag="maskb")
+        nc.vector.tensor_scalar(out=maskb[:], in0=ident[:, P - 1 : P], scalar1=-30000.0, scalar2=None, op0=ALU.mult)
 
         xb = []
         for i in range(2):
@@ -94,7 +98,6 @@ def tile_minibatchdiscriminator_kernel(tc, tensor, T, out_0, out_1):
         for par in range(2):
             hnp = keep.tile([P, FXW], F32, name="hn%d" % par, tag="hn%d" % par)
             hns.append(hnp)
-        maskb = keep.tile([P, 1], F32, name="maskb", tag="maskb")
         xmax = keep.tile([P, 2], F32, name="xmax", tag="xmax")
         xq = keep.tile([P, 4 * N_ROWS], U32, name="xq", tag="xq", align_bytes=64)
         xs = keep.tile([P, 4 * N_ROWS], U8, name="xs", tag="xs", align_bytes=64)
@@ -150,55 +153,43 @@ def tile_minibatchdiscriminator_kernel(tc, tensor, T, out_0, out_1):
                 nc.vector.tensor_copy(out=tg[:, 0:512, :], in_=raw[:, :, 0:512].rearrange("p t w -> p w t"))
                 nc.scalar.copy(out=tg[:, 512:1024, :], in_=raw[:, :, 512:1024].rearrange("p t w -> p w t"))
 
-            def quantise_and_multiply(q):
+            def quantise_and_multiply(q, parts):
                 c, h = divmod(q, 2)
-                cols = slice(1024 * h, 1024 * (h + 1))
-                nc.vector.quantize_mx(
-                    out=tq[:, c, cols].bitcast(FP8X4),
-                    scales=ts[:, c, cols],
-                    in_=tgs[q][:].rearrange("p w t -> p (w t)"),
-                )
-                for wq in (2 * h, 2 * h + 1):
-                    for i in range(2):
-                        n_cols = slice(256 * c + P * i, 256 * c + P * (i + 1))
-                        w_cols = slice(512 * wq, 512 * (wq + 1))
-                        nc.tensor.matmul_mx(
-                            out=fb[(i, wq)][:],
-                            lhsT=xq[:, n_cols].bitcast(FP8X4),
-                            lhsT_scale=xs[:, n_cols],
-                            rhs=tq[:, c, w_cols].bitcast(FP8X4),
-                            rhs_scale=ts[:, c, w_cols],
-                            start=(c == 0),
-                            stop=(c == 3),
-                        )
+                width = 1024 // parts
+                for part in range(parts):
+                    first = 1024 * h + width * part
+                    nc.vector.quantize_mx(
+                        out=tq[:, c, first : first + width].bitcast(FP8X4),
+                        scales=ts[:, c, first : first + width],
+                        in_=tgs[q][:, width * part : width * (part + 1), :].rearrange("p w t -> p (w t)"),
+                    )
+                    for wq in range(first // 512, (first + width) // 512):
+                        for i in range(2):
+                            n_cols = slice(256 * c + P * i, 256 * c + P * (i + 1))
+                            w_cols = slice(512 * wq, 512 * (wq + 1))
+                            nc.tensor.matmul_mx(
+                                out=fb[(i, wq)][:],
+                                lhsT=xq[:, n_cols].bitcast(FP8X4),
+                                lhsT_scale=xs[:, n_cols],
+                                rhs=tq[:, c, w_cols].bitcast(FP8X4),
+                                rhs_scale=ts[:, c, w_cols],
+                                start=(c == 0),
+                                stop=(c == 3),
+                            )
 
             for q in range(9):
                 if q < 8:
                     interleave(q)
                 if q >= 1:
-                    quantise_and_multiply(q - 1)
+                    quantise_and_multiply(q - 1, 2 if q == 8 else 1)
 
-        for i in range(2):
-            for wq in range(4):
-                dst = fsb[i][:, :, 32 * wq : 32 * (wq + 1)]
-                src = fb[(i, wq)][:].rearrange("p (j k) -> p k j", k=KD)
-                if wq % 2 == 0:
-                    nc.vector.tensor_copy(out=dst, in_=src)
-                else:
-                    nc.scalar.copy(out=dst, in_=src)
-
-        for kp in range(8):
-            pk = bank(kp, [P, 2, N_ROWS], "pk")
-            for kk in range(2):
-                for i in range(2):
-                    nc.tensor.transpose(pk[:, kk, i * P : (i + 1) * P], fsb[i][:, 2 * kp + kk, :], ident[:])
-            for kk in range(2):
-                k = 2 * kp + kk
-                if k < S_MAX:
-                    nc.scalar.activation(out=fx[:, k, 0:N_ROWS], in_=pk[:, kk, :], func=ACT.Copy, scale=0.5)
-                if k >= S_MAX - 1:
-                    plane = KD if k == S_MAX - 1 else k
-                    nc.vector.tensor_copy(out=fx[:, plane, 0:N_ROWS], in_=pk[:, kk, :])
+        for eng, i, wq in (("s", 0, 0), ("s", 0, 1), ("s", 1, 0), ("s", 1, 1), ("v", 0, 2), ("v", 1, 2), ("s", 0, 3), ("v", 1, 3)):
+            dst = fsb[i][:, :, 32 * wq : 32 * (wq + 1)]
+            src = fb[(i, wq)][:].rearrange("p (j k) -> p k j", k=KD)
+            if eng == "v":
+                nc.vector.tensor_copy(out=dst, in_=src)
+            else:
+                nc.scalar.copy(out=dst, in_=src)
 
         hp = bank(0, [P, N_ROWS], "hp")
         vec_ks = list(range(S_MAX, KD))
@@ -213,8 +204,23 @@ def tile_minibatchdiscriminator_kernel(tc, tensor, T, out_0, out_1):
                     stop=(idx == len(vec_ks) - 1),
                 )
         nc.vector.tensor_scalar(out=hns[0][:, 0:N_ROWS], in0=hp[:], scalar1=-0.5, scalar2=None, op0=ALU.mult)
+
+        for kp in TURN_ORDER:
+            pk = bank(kp, [P, 2, N_ROWS], "pk")
+            for kk in range(2):
+                for i in range(2):
+                    nc.tensor.transpose(pk[:, kk, i * P : (i + 1) * P], fsb[i][:, 2 * kp + kk, :], ident[:])
+            for kk in range(2):
+                k = 2 * kp + kk
+                if k < S_MAX:
+                    nc.scalar.activation(out=fx[:, k, 0:N_ROWS], in_=pk[:, kk, :], func=ACT.Copy, scale=0.5)
+                if k >= S_MAX - 1:
+                    plane = KD if k == S_MAX - 1 else k
+                    if k in V_COPIES:
+                        nc.vector.tensor_copy(out=fx[:, plane, 0:N_ROWS], in_=pk[:, kk, :])
+                    else:
+                        nc.scalar.copy(out=fx[:, plane, 0:N_ROWS], in_=pk[:, kk, :])
         nc.vector.tensor_tensor(out=hns[1][:, 0:N_ROWS], in0=hns[0][:, 0:N_ROWS], in1=fx[:, S_MAX - 1, 0:N_ROWS], op=ALU.subtract)
-        nc.vector.tensor_scalar(out=maskb[:], in0=ident[:, P - 1 : P], scalar1=-30000.0, scalar2=None, op0=ALU.mult)
 
         rb = bank(5, [P, N_ROWS + ONES_W], "rb")
         c_even = bank(6, [P, FXW], "c_even")
@@ -245,6 +251,12 @@ def tile_minibatchdiscriminator_kernel(tc, tensor, T, out_0, out_1):
         vap = ctx.enter_context(tc.tile_pool(name="vap", bufs=4))
         epl = ctx.enter_context(tc.tile_pool(name="epl", bufs=3))
         fin = ctx.enter_context(tc.tile_pool(name="fin", bufs=1))
+        ce_sb = fin.tile([P, FXW], F32, name="ce_sb", tag="ce_sb")
+        co_sb = fin.tile([P, FXW], F32, name="co_sb", tag="co_sb")
+        rb_sb = fin.tile([P, N_ROWS], F32, name="rb_sb", tag="rb_sb")
+        xrcp = fin.tile([P, 2], F32, name="xrcp", tag="xrcp")
+        xfac = fin.tile([P, 2], F32, name="xfac", tag="xfac")
+        nc.vector.memset(co_sb[:, 0:1], 0.0)
         sas, vas, lbs, ets = {}, {}, {}, {}
 
         def scalar_row(m):
@@ -346,12 +358,12 @@ def tile_minibatchdiscriminator_kernel(tc, tensor, T, out_0, out_1):
                 nc.vector.tensor_copy(out=hnp[:, N_ROWS:FXW], in_=hnp[:, 0:WIN])
             vector_slot(t)
             if t == N_ROWS:
-                nc.vector.tensor_copy(out=o32[1][:, 0:IN_F], in_=xb[1][:])
-                nc.sync.dma_start(out=out_0[P : 2 * P, 0:IN_F], in_=o32[1][:, 0:IN_F])
                 for i in range(2):
                     nc.vector.tensor_reduce(
                         out=xmax[:, i : i + 1], in_=xb[i][:], axis=AX.X, op=ALU.max, apply_absolute_value=True
                     )
+                nc.vector.reciprocal(out=xrcp[:], in_=xmax[:])
+                nc.vector.tensor_scalar(out=xfac[:], in0=xrcp[:], scalar1=448.0, scalar2=None, op0=ALU.mult)
             if 0 < t < N_ROWS - R and (t + R) % (R * KICK_EVERY) == 0:
                 kick(KICK)
             if 0 <= t < N_ROWS:
@@ -364,36 +376,39 @@ def tile_minibatchdiscriminator_kernel(tc, tensor, T, out_0, out_1):
             if t % R == R - 1 and 0 <= t // R - 1 < GROUPS:
                 expo(t // R - 1)
             if t == N_ROWS - 1:
-                nc.scalar.copy(out=o32[0][:, 0:IN_F], in_=xb[0][:])
-                nc.sync.dma_start(out=out_0[0:P, 0:IN_F], in_=o32[0][:, 0:IN_F])
+                for i in range(2):
+                    nc.scalar.copy(out=o32[i][:, 0:IN_F], in_=xb[i][:])
+                    nc.sync.dma_start(out=out_0[i * P : (i + 1) * P, 0:IN_F], in_=o32[i][:, 0:IN_F])
 
-        dv = fin.tile([P, N_ROWS], F32, name="dv", tag="dv")
-        nc.vector.tensor_scalar(out=dv[:], in0=rb[:, 0:N_ROWS], scalar1=1.0, scalar2=None, op0=ALU.add)
-        nc.vector.tensor_tensor(out=dv[:], in0=c_even[:, 0:N_ROWS], in1=dv[:], op=ALU.add)
-        nc.vector.tensor_tensor(out=dv[:, 0:WIN], in0=c_even[:, N_ROWS:FXW], in1=dv[:, 0:WIN], op=ALU.add)
-        nc.vector.tensor_tensor(out=dv[:, 1:N_ROWS], in0=c_odd[:, 0 : N_ROWS - 1], in1=dv[:, 1:N_ROWS], op=ALU.add)
-        nc.vector.tensor_tensor(out=dv[:, 0:WIN], in0=c_odd[:, N_ROWS - 1 : FXW - 1], in1=dv[:, 0:WIN], op=ALU.add)
+        nc.vector.tensor_copy(out=ce_sb[:], in_=c_even[:])
+        nc.scalar.copy(out=co_sb[:, 1:FXW], in_=c_odd[:, 0 : FXW - 1])
+        nc.scalar.copy(out=rb_sb[:], in_=rb[:, 0:N_ROWS])
         dt_ps = bank(0, [P, 2, J], "dt_ps")
         dmax = fin.tile([P, 2], F32, name="dmax", tag="dmax")
         for i in range(2):
-            nc.tensor.transpose(dt_ps[:, i, :], dv[:, i * P : (i + 1) * P], ident[:])
+            pieces = [ce_sb[:, i * P : (i + 1) * P], co_sb[:, i * P : (i + 1) * P]]
+            if i == 0:
+                pieces.extend([ce_sb[:, N_ROWS:FXW], co_sb[:, N_ROWS:FXW]])
+            pieces.append(rb_sb[:, i * P : (i + 1) * P])
+            for idx, piece in enumerate(pieces):
+                nc.tensor.matmul(
+                    out=dt_ps[:, i, :], lhsT=piece, rhs=ident[:], is_transpose=True, start=(idx == 0), stop=(idx == len(pieces) - 1)
+                )
         for i in range(2):
             nc.vector.tensor_scalar(
                 out=o32[i][:, IN_F:OUT_W],
                 in0=dt_ps[:, i, :],
                 scalar1=1.0,
                 scalar2=None,
-                op0=ALU.mult,
+                op0=ALU.add,
                 op1=ALU.max,
                 accum_out=dmax[:, i : i + 1],
             )
             nc.sync.dma_start(out=out_0[i * P : (i + 1) * P, IN_F:OUT_W], in_=o32[i][:, IN_F:OUT_W])
-        amax = fin.tile([P, 2], F32, name="amax", tag="amax")
-        nc.vector.tensor_tensor(out=amax[:], in0=dmax[:], in1=xmax[:], op=ALU.max)
         rcp = fin.tile([P, 2], F32, name="rcp", tag="rcp")
-        nc.vector.reciprocal(out=rcp[:], in_=amax[:])
+        nc.vector.reciprocal(out=rcp[:], in_=dmax[:])
         fac = fin.tile([P, 2], F32, name="fac", tag="fac")
-        nc.vector.tensor_scalar(out=fac[:], in0=rcp[:], scalar1=448.0, scalar2=None, op0=ALU.mult)
+        nc.vector.scalar_tensor_tensor(out=fac[:], in0=rcp[:], scalar=448.0, in1=xfac[:], op0=ALU.mult, op1=ALU.min)
         for i in range(2):
             rows = slice(i * P, (i + 1) * P)
             o8v = fin.tile([P, CAST_SPLIT], FP8, name="o8v%d" % i, tag="o8v%d" % i)

@@ -34,7 +34,8 @@ FXW = N_ROWS + WIN
 L_BANKS = 4
 TURN_ORDER = (5, 4, 3, 6, 7, 0, 1, 2)
 V_COPIES = (8, 9, 10, 11)
-FIRST_KICK = 4
+BRIDGE_KICK = 4
+FIRST_KICK = 8
 KICK_EVERY = 16
 KICK = 4
 IDLE_TURNS = 3
@@ -101,6 +102,18 @@ def tile_minibatchdiscriminator_kernel(tc, tensor, T, out_0, out_1):
         xmax = keep.tile([P, 2], F32, name="xmax", tag="xmax")
         xq = keep.tile([P, 4 * N_ROWS], U32, name="xq", tag="xq", align_bytes=64)
         xs = keep.tile([P, 4 * N_ROWS], U8, name="xs", tag="xs", align_bytes=64)
+
+        def kick(unread, passes):
+            for rep in range(passes):
+                nc.tensor.matmul_mx(
+                    out=unread[:],
+                    lhsT=xq[:, 0:P].bitcast(FP8X4),
+                    lhsT_scale=xs[:, 0:P],
+                    rhs=xq[:, 0:512].bitcast(FP8X4),
+                    rhs_scale=xs[:, 0:512],
+                    start=True,
+                    stop=True,
+                )
 
         fb = {}
         with tc.tile_pool(name="ph1", bufs=1) as ph1:
@@ -190,6 +203,8 @@ def tile_minibatchdiscriminator_kernel(tc, tensor, T, out_0, out_1):
                 nc.vector.tensor_copy(out=dst, in_=src)
             else:
                 nc.scalar.copy(out=dst, in_=src)
+            if (i, wq) == (0, 0):
+                kick(bank(0, [P, 512], "idle"), BRIDGE_KICK)
 
         hp = bank(0, [P, N_ROWS], "hp")
         vec_ks = list(range(S_MAX, KD))
@@ -232,20 +247,7 @@ def tile_minibatchdiscriminator_kernel(tc, tensor, T, out_0, out_1):
                 )
 
         scratch = bank(4, [P, 512], "scratch")
-
-        def kick(passes):
-            for rep in range(passes):
-                nc.tensor.matmul_mx(
-                    out=scratch[:],
-                    lhsT=xq[:, 0:P].bitcast(FP8X4),
-                    lhsT_scale=xs[:, 0:P],
-                    rhs=xq[:, 0:512].bitcast(FP8X4),
-                    rhs_scale=xs[:, 0:512],
-                    start=True,
-                    stop=True,
-                )
-
-        kick(FIRST_KICK)
+        kick(scratch, FIRST_KICK)
 
         sap = ctx.enter_context(tc.tile_pool(name="sap", bufs=3))
         vap = ctx.enter_context(tc.tile_pool(name="vap", bufs=4))
@@ -365,7 +367,7 @@ def tile_minibatchdiscriminator_kernel(tc, tensor, T, out_0, out_1):
                 nc.vector.reciprocal(out=xrcp[:], in_=xmax[:])
                 nc.vector.tensor_scalar(out=xfac[:], in0=xrcp[:], scalar1=448.0, scalar2=None, op0=ALU.mult)
             if 0 < t < N_ROWS - R and (t + R) % (R * KICK_EVERY) == 0:
-                kick(KICK)
+                kick(scratch, KICK)
             if 0 <= t < N_ROWS:
                 accumulate_row(t)
             if 0 <= t < 2 * R:

@@ -18,24 +18,27 @@ AX = mybir.AxisListType
 
 P = 128
 R = 4
-S_ROW = (7, 7, 7, 6)
-CHAIN_ROW = (5, 6, 5, 6)
+S_ROW = (6, 6, 6, 6)
+CHAIN_ROW = (7, 7, 7, 8)
+G_ROW = tuple([KD - S_ROW[r] - CHAIN_ROW[r] for r in range(R)])
+G_STARTS = (False, False, False, True)
 S_MAX = max(S_ROW)
-W_MAX = max([KD - S_ROW[r] - CHAIN_ROW[r] for r in range(R)])
+S_MIN = min(S_ROW)
+G_MAX = max(G_ROW)
 C_MAX = max(CHAIN_ROW)
-OWN_AHEAD = 1
-FIRST_ROWS = 2
-FIRST_AHEAD = C_MAX - 2
-PLANES = KD + 1
+PLANES = S_MAX + KD - S_MIN
+LOOPED = S_MAX + KD - min(CHAIN_ROW) - S_MIN
+S_AHEAD = R
+G_AHEAD = 2
+START_AHEAD = C_MAX + 1
+FLT_BIG = 3.0e38
 ONES_W = 24
 GROUPS = N_ROWS // R
 WIN = 128
 FXW = N_ROWS + WIN
-L_BANKS = 4
-TURN_ORDER = (5, 4, 3, 6, 7, 0, 1, 2)
-V_COPIES = (8, 9, 10, 11)
+L_BANKS = 2
 BRIDGE_KICK = 4
-FIRST_KICK = 8
+FIRST_KICK = 16
 KICK_EVERY = 16
 KICK = 4
 IDLE_TURNS = 3
@@ -47,20 +50,20 @@ def tile_minibatchdiscriminator_kernel(tc, tensor, T, out_0, out_1):
     nc = tc.nc
     t_mat = T.rearrange("i j k -> i (j k)")
 
-    def scalar_planes(m):
-        return list(range(S_ROW[m % R]))
+    def whole(k):
+        return S_MAX + k - S_MIN
 
-    def vector_planes(m):
-        return [KD if k == S_MAX - 1 else k for k in range(S_ROW[m % R], KD)]
+    def scalar_ks(m):
+        return range(S_ROW[m % R])
 
-    def own_planes(m):
-        return vector_planes(m)[: KD - S_ROW[m % R] - CHAIN_ROW[m % R]]
+    def gpsimd_ks(m):
+        return range(S_ROW[m % R], S_ROW[m % R] + G_ROW[m % R])
 
-    def chain_planes(m):
-        return vector_planes(m)[KD - S_ROW[m % R] - CHAIN_ROW[m % R] :]
+    def chain_start(m):
+        return C_MAX - CHAIN_ROW[m % R]
 
-    def hn_of(m):
-        return hns[S_MAX - S_ROW[m % R]]
+    def chain_k(place):
+        return KD - C_MAX + place
 
     with ExitStack() as ctx:
         ctx.enter_context(tc.manual_schedule())
@@ -74,8 +77,9 @@ def tile_minibatchdiscriminator_kernel(tc, tensor, T, out_0, out_1):
         make_identity(nc, ident[:])
         zeros = keep.tile([P, P], F32, name="zeros", tag="zeros")
         nc.vector.memset(zeros[:], 0.0)
-        ones = keep.tile([P, ONES_W], F32, name="ones", tag="ones")
-        nc.vector.memset(ones[:], 1.0)
+        ones = keep.tile([P, 2 * ONES_W], F32, name="ones", tag="ones")
+        nc.vector.memset(ones[:], 0.0)
+        nc.vector.memset(ones[:, ONES_W - 1 : ONES_W], 1.0)
         warm = keep.tile([P, 1], F32, name="warm", tag="warm")
         nc.scalar.activation(out=warm[:], in_=zeros[:, 0:1], func=ACT.Exp)
         maskb = keep.tile([P, 1], F32, name="maskb", tag="maskb")
@@ -95,10 +99,7 @@ def tile_minibatchdiscriminator_kernel(tc, tensor, T, out_0, out_1):
             fsbi = keep.tile([P, KD, J], F32, name="fsb%d" % i, tag="fsb%d" % i)
             fsb.append(fsbi)
         fx = keep.tile([P, PLANES, FXW], F32, name="fx", tag="fx")
-        hns = []
-        for par in range(2):
-            hnp = keep.tile([P, FXW], F32, name="hn%d" % par, tag="hn%d" % par)
-            hns.append(hnp)
+        hn = keep.tile([P, FXW], F32, name="hn", tag="hn")
         xmax = keep.tile([P, 2], F32, name="xmax", tag="xmax")
         xq = keep.tile([P, 4 * N_ROWS], U32, name="xq", tag="xq", align_bytes=64)
         xs = keep.tile([P, 4 * N_ROWS], U8, name="xs", tag="xs", align_bytes=64)
@@ -206,130 +207,135 @@ def tile_minibatchdiscriminator_kernel(tc, tensor, T, out_0, out_1):
             if (i, wq) == (0, 0):
                 kick(bank(0, [P, 512], "idle"), BRIDGE_KICK)
 
-        hp = bank(0, [P, N_ROWS], "hp")
-        vec_ks = list(range(S_MAX, KD))
+        hp = bank(6, [P, N_ROWS], "hp")
         for i in range(2):
-            for idx, k in enumerate(vec_ks):
+            for k in range(S_MIN, KD):
                 nc.tensor.matmul(
                     out=hp[:, i * P : (i + 1) * P],
                     lhsT=fsb[i][:, k, :],
                     rhs=ident[:],
                     is_transpose=True,
-                    start=(idx == 0),
-                    stop=(idx == len(vec_ks) - 1),
+                    start=(k == S_MIN),
+                    stop=(k == KD - 1),
                 )
-        nc.vector.tensor_scalar(out=hns[0][:, 0:N_ROWS], in0=hp[:], scalar1=-0.5, scalar2=None, op0=ALU.mult)
+        nc.vector.tensor_scalar(out=hn[:, 0:N_ROWS], in0=hp[:], scalar1=-0.5, scalar2=None, op0=ALU.mult)
 
-        for kp in TURN_ORDER:
-            pk = bank(kp, [P, 2, N_ROWS], "pk")
+        vps = []
+        for b in range(C_MAX // 2):
+            vps.append(bank(b, [P, 2, N_ROWS], "vp%d" % b))
+
+        def turn_chain_plane(place, first):
+            for half in range(2):
+                i = (first + half) % 2
+                nc.tensor.transpose(
+                    vps[place // 2][:, place % 2, half * P : (half + 1) * P], fsb[i][:, chain_k(place), :], ident[:]
+                )
+
+        def turn_pair(k, b):
+            pk = bank(b, [P, 2, N_ROWS], "pk")
             for kk in range(2):
                 for i in range(2):
-                    nc.tensor.transpose(pk[:, kk, i * P : (i + 1) * P], fsb[i][:, 2 * kp + kk, :], ident[:])
+                    nc.tensor.transpose(pk[:, kk, i * P : (i + 1) * P], fsb[i][:, k + kk, :], ident[:])
+            return pk
+
+        for b in range(C_MAX // 2):
             for kk in range(2):
-                k = 2 * kp + kk
-                if k < S_MAX:
-                    nc.scalar.activation(out=fx[:, k, 0:N_ROWS], in_=pk[:, kk, :], func=ACT.Copy, scale=0.5)
-                if k >= S_MAX - 1:
-                    plane = KD if k == S_MAX - 1 else k
-                    if k in V_COPIES:
-                        nc.vector.tensor_copy(out=fx[:, plane, 0:N_ROWS], in_=pk[:, kk, :])
-                    else:
-                        nc.scalar.copy(out=fx[:, plane, 0:N_ROWS], in_=pk[:, kk, :])
-        nc.vector.tensor_tensor(out=hns[1][:, 0:N_ROWS], in0=hns[0][:, 0:N_ROWS], in1=fx[:, S_MAX - 1, 0:N_ROWS], op=ALU.subtract)
+                turn_chain_plane(2 * b + kk, 0)
+            k = chain_k(2 * b)
+            nc.vector.tensor_copy(out=fx[:, whole(k) : whole(k) + 2, 0:N_ROWS], in_=vps[b][:])
+            if 2 * b < S_MAX:
+                pk = turn_pair(2 * b, (5, 7, 6)[b])
+                nc.scalar.activation(out=fx[:, 2 * b : 2 * b + 2, 0:N_ROWS], in_=pk[:], func=ACT.Copy, scale=0.5)
+        pk = turn_pair(S_MIN, 7)
+        nc.scalar.copy(out=fx[:, whole(S_MIN) : whole(S_MIN) + 2, 0:N_ROWS], in_=pk[:])
+        nc.sync.dma_start(out=hn[:, N_ROWS:FXW], in_=hn[:, 0:WIN])
+        nc.sync.dma_start(out=fx[:, 0:LOOPED, N_ROWS:FXW], in_=fx[:, 0:LOOPED, 0:WIN])
 
-        rb = bank(5, [P, N_ROWS + ONES_W], "rb")
-        c_even = bank(6, [P, FXW], "c_even")
-        c_odd = bank(7, [P, FXW], "c_odd")
-        for cb in (c_even, c_odd):
-            for z in range(3):
-                nc.tensor.matmul(
-                    out=cb[:, z * P : (z + 1) * P], lhsT=zeros[:], rhs=ident[:], is_transpose=True, start=(z == 0), stop=False
-                )
-
-        scratch = bank(4, [P, 512], "scratch")
-        kick(scratch, FIRST_KICK)
+        kick(bank(4, [P, 512], "idle"), FIRST_KICK)
 
         sap = ctx.enter_context(tc.tile_pool(name="sap", bufs=3))
-        vap = ctx.enter_context(tc.tile_pool(name="vap", bufs=4))
+        gap = ctx.enter_context(tc.tile_pool(name="gap", bufs=3))
+        vap = ctx.enter_context(tc.tile_pool(name="vap", bufs=5))
         epl = ctx.enter_context(tc.tile_pool(name="epl", bufs=3))
         fin = ctx.enter_context(tc.tile_pool(name="fin", bufs=1))
-        ce_sb = fin.tile([P, FXW], F32, name="ce_sb", tag="ce_sb")
-        co_sb = fin.tile([P, FXW], F32, name="co_sb", tag="co_sb")
-        rb_sb = fin.tile([P, N_ROWS], F32, name="rb_sb", tag="rb_sb")
+        ca_sb = fin.tile([P, FXW + P], F32, name="ca_sb", tag="ca_sb")
+        cb_sb = fin.tile([P, FXW], F32, name="cb_sb", tag="cb_sb")
+        rb_sb = fin.tile([P, P], F32, name="rb_sb", tag="rb_sb")
         xrcp = fin.tile([P, 2], F32, name="xrcp", tag="xrcp")
         xfac = fin.tile([P, 2], F32, name="xfac", tag="xfac")
-        nc.vector.memset(co_sb[:, 0:1], 0.0)
-        sas, vas, lbs, ets = {}, {}, {}, {}
+        nc.vector.memset(cb_sb[:, 0:1], 0.0)
+        sas, gas, vas, lbs, ets, accs = {}, {}, {}, {}, {}, {}
+
+        def group_tile(tiles, pool, m, count, name):
+            g = m // R
+            if g not in tiles:
+                made = pool.tile([P, R, count, WIN], F32, name=name, tag=name)
+                tiles[g] = made
+            return tiles[g]
 
         def scalar_row(m):
-            g, r = divmod(m, R)
-            if r == 0:
-                sa = sap.tile([P, R, S_MAX, WIN], F32, name="sa", tag="sa")
-                sas[g] = sa
-            for idx, k in enumerate(scalar_planes(m)):
+            sa = group_tile(sas, sap, m, S_MAX, "sa")
+            for idx, k in enumerate(scalar_ks(m)):
                 nc.scalar.activation(
-                    out=sas[g][:, r, idx, :], in_=fx[:, k, m + 1 : m + 1 + WIN], func=ACT.Abs, scale=-1.0, bias=fx[:, k, m : m + 1]
+                    out=sa[:, m % R, idx, :], in_=fx[:, k, m + 1 : m + 1 + WIN], func=ACT.Abs, scale=-1.0, bias=fx[:, k, m : m + 1]
                 )
 
-        def vector_tiles(m):
-            g = m // R
-            if g not in vas:
-                va = vap.tile([P, R, W_MAX + 1, WIN], F32, name="va", tag="va")
-                vas[g] = va
-            return vas[g]
+        def gpsimd_row(m):
+            ga = group_tile(gas, gap, m, G_MAX, "ga")
+            for idx, k in enumerate(gpsimd_ks(m)):
+                nc.gpsimd.tensor_scalar(
+                    out=ga[:, m % R, idx, :],
+                    in0=fx[:, whole(k), m + 1 : m + 1 + WIN],
+                    scalar1=FLT_BIG,
+                    scalar2=fx[:, whole(k), m : m + 1],
+                    op0=ALU.min,
+                    op1=ALU.max,
+                )
 
-        def own_tile(m, idx):
-            va = vector_tiles(m)
-            k = own_planes(m)[idx]
-            if idx == 0:
+        def gpsimd_start(m):
+            va = group_tile(vas, vap, m, 1, "va")
+            nc.gpsimd.tensor_scalar(
+                out=va[:, m % R, 0, :],
+                in0=hn[:, m + 1 : m + 1 + WIN],
+                scalar1=1.0,
+                scalar2=hn[:, m : m + 1],
+                op0=ALU.mult,
+                op1=ALU.add,
+            )
+
+        def chain_link(m, place):
+            chain = group_tile(vas, vap, m, 1, "va")[:, m % R, 0, :]
+            k = chain_k(place)
+            plane = vps[place // 2][:, place % 2, m % P + 1 : m % P + 1 + WIN]
+            if place == chain_start(m) and not G_STARTS[m % R]:
                 nc.vector.tensor_scalar(
-                    out=va[:, m % R, idx, :],
-                    in0=fx[:, k, m + 1 : m + 1 + WIN],
-                    scalar1=fx[:, k, m : m + 1],
-                    scalar2=hn_of(m)[:, m : m + 1],
+                    out=chain,
+                    in0=plane,
+                    scalar1=fx[:, whole(k), m : m + 1],
+                    scalar2=hn[:, m : m + 1],
                     op0=ALU.max,
                     op1=ALU.add,
                 )
             else:
-                nc.vector.tensor_scalar(
-                    out=va[:, m % R, idx, :],
-                    in0=fx[:, k, m + 1 : m + 1 + WIN],
-                    scalar1=fx[:, k, m : m + 1],
-                    scalar2=None,
-                    op0=ALU.max,
+                nc.vector.scalar_tensor_tensor(
+                    out=chain, in0=plane, scalar=fx[:, whole(k), m : m + 1], in1=chain, op0=ALU.max, op1=ALU.add
                 )
-
-        def chain_link(m, idx):
-            va = vector_tiles(m)
-            k = chain_planes(m)[idx]
-            nc.vector.scalar_tensor_tensor(
-                out=va[:, m % R, W_MAX, :],
-                in0=fx[:, k, m + 1 : m + 1 + WIN],
-                scalar=fx[:, k, m : m + 1],
-                in1=(hn_of(m)[:, m + 1 : m + 1 + WIN] if idx == 0 else va[:, m % R, W_MAX, :]),
-                op0=ALU.max,
-                op1=ALU.add,
-            )
 
         def vector_slot(t):
             for d in range(C_MAX):
                 m = t + d
-                if 0 <= m < N_ROWS and CHAIN_ROW[m % R] - 1 - d >= 0:
-                    chain_link(m, CHAIN_ROW[m % R] - 1 - d)
-            for ahead in (OWN_AHEAD, FIRST_AHEAD):
-                m = t + ahead
-                if 0 <= m < N_ROWS and (m < FIRST_ROWS) == (ahead == FIRST_AHEAD):
-                    for idx in range(len(own_planes(m))):
-                        own_tile(m, idx)
+                place = C_MAX - 1 - d
+                if 0 <= m < N_ROWS and place >= chain_start(m):
+                    chain_link(m, place)
 
         def accumulate_row(m):
             g, r = divmod(m, R)
-            if r == 0:
-                lbs[g] = bank(g % L_BANKS, [P, R, J], "lb")
             lb = lbs[g]
-            srcs = [sas[g][:, r, idx, :] for idx in range(len(scalar_planes(m)))]
-            srcs.extend([vas[g][:, r, idx, :] for idx in range(len(own_planes(m)))])
-            srcs.append(vas[g][:, r, W_MAX, :])
+            srcs = [sas[g][:, r, idx, :] for idx in range(S_ROW[r])]
+            if not G_STARTS[r]:
+                srcs.append(hn[:, m + 1 : m + 1 + WIN])
+            srcs.extend([gas[g][:, r, idx, :] for idx in range(G_ROW[r])])
+            srcs.append(vas[g][:, r, 0, :])
             for idx, src in enumerate(srcs):
                 nc.tensor.matmul(
                     out=lb[:, r, :], lhsT=src, rhs=ident[:], is_transpose=True, start=(idx == 0), stop=(idx == len(srcs) - 1)
@@ -343,21 +349,29 @@ def tile_minibatchdiscriminator_kernel(tc, tensor, T, out_0, out_1):
 
         def fold_row(m):
             g, r = divmod(m, R)
-            if m % 2 == 1:
-                dst = c_even[:, m + 1 : m + 1 + WIN]
-            else:
-                dst = c_odd[:, m : m + WIN]
-            nc.tensor.matmul(out=dst, lhsT=ets[g][:, r, :], rhs=ident[:], is_transpose=True, start=False, stop=(m >= N_ROWS - 2))
-            nc.tensor.matmul(out=rb[:, m : m + ONES_W], lhsT=ets[g][:, r, :], rhs=ones[:], start=True, stop=True)
+            odd = m % 2
+            first = m + 1 if odd else m
+            nc.tensor.matmul(
+                out=accs[odd][:, first : first + WIN], lhsT=ets[g][:, r, :], rhs=ident[:], is_transpose=True, start=False, stop=(m == N_ROWS - 1)
+            )
+            half, col = divmod(m, P)
+            left = min(col - col % 2, P - ONES_W)
+            skip = ONES_W - 1 - (col - left)
+            nc.tensor.matmul(
+                out=accs[1 - half][:, FXW + left : FXW + left + ONES_W],
+                lhsT=ets[g][:, r, :],
+                rhs=ones[:, skip : skip + ONES_W],
+                start=False,
+                stop=(m == N_ROWS - 1),
+            )
 
-        for t in range(-C_MAX, N_ROWS + 2 * R):
-            if 0 <= t + R < N_ROWS:
-                scalar_row(t + R)
-            if t % R == 0 and 8 <= t // R < 8 + PLANES:
-                nc.vector.tensor_copy(out=fx[:, t // R - 8, N_ROWS:FXW], in_=fx[:, t // R - 8, 0:WIN])
-            if t % R == 0 and 8 + PLANES <= t // R < 10 + PLANES:
-                hnp = hns[t // R - 8 - PLANES]
-                nc.vector.tensor_copy(out=hnp[:, N_ROWS:FXW], in_=hnp[:, 0:WIN])
+        for t in range(-START_AHEAD, N_ROWS + 2 * R):
+            if 0 <= t + S_AHEAD < N_ROWS:
+                scalar_row(t + S_AHEAD)
+            if 0 <= t + START_AHEAD < N_ROWS and G_STARTS[(t + START_AHEAD) % R]:
+                gpsimd_start(t + START_AHEAD)
+            if 0 <= t + G_AHEAD < N_ROWS:
+                gpsimd_row(t + G_AHEAD)
             vector_slot(t)
             if t == N_ROWS:
                 for i in range(2):
@@ -366,32 +380,45 @@ def tile_minibatchdiscriminator_kernel(tc, tensor, T, out_0, out_1):
                     )
                 nc.vector.reciprocal(out=xrcp[:], in_=xmax[:])
                 nc.vector.tensor_scalar(out=xfac[:], in0=xrcp[:], scalar1=448.0, scalar2=None, op0=ALU.mult)
-            if 0 < t < N_ROWS - R and (t + R) % (R * KICK_EVERY) == 0:
-                kick(scratch, KICK)
-            if 0 <= t < N_ROWS:
-                accumulate_row(t)
+            if 0 <= t < N_ROWS and t % R == 0:
+                g = t // R
+                lbs[g] = bank(4 + g % L_BANKS, [P, R, J], "lb")
+                if g > 0 and g % KICK_EVERY == 0:
+                    kick(lbs[g][:].rearrange("p r j -> p (r j)"), KICK)
             if 0 <= t < 2 * R:
                 for rep in range(IDLE_TURNS):
-                    nc.tensor.transpose(scratch[:, 0:P], ident[:], ident[:])
+                    nc.tensor.transpose(lbs[t // R][:, t % R, :], ident[:], ident[:])
+            if 0 <= t < N_ROWS:
+                accumulate_row(t)
+            if t == R:
+                for odd in range(2):
+                    acc = bank(6 + odd, [P, FXW + P], "acc")
+                    accs[1 - odd] = acc
+                    for z in range(R):
+                        nc.tensor.matmul(
+                            out=acc[:, z * P : (z + 1) * P], lhsT=zeros[:], rhs=ident[:], is_transpose=True, start=(z == 0), stop=False
+                        )
+            if 0 <= t - (P - C_MAX) < C_MAX:
+                turn_chain_plane(t - (P - C_MAX), 1)
             if 0 <= t - 2 * R < N_ROWS:
                 fold_row(t - 2 * R)
-            if t % R == R - 1 and 0 <= t // R - 1 < GROUPS:
+            if t % R == 1 and 0 <= t // R - 1 < GROUPS:
                 expo(t // R - 1)
             if t == N_ROWS - 1:
                 for i in range(2):
                     nc.scalar.copy(out=o32[i][:, 0:IN_F], in_=xb[i][:])
                     nc.sync.dma_start(out=out_0[i * P : (i + 1) * P, 0:IN_F], in_=o32[i][:, 0:IN_F])
 
-        nc.vector.tensor_copy(out=ce_sb[:], in_=c_even[:])
-        nc.scalar.copy(out=co_sb[:, 1:FXW], in_=c_odd[:, 0 : FXW - 1])
-        nc.scalar.copy(out=rb_sb[:], in_=rb[:, 0:N_ROWS])
+        nc.vector.tensor_copy(out=ca_sb[:], in_=accs[1][:])
+        nc.scalar.copy(out=cb_sb[:, 1:FXW], in_=accs[0][:, 0 : FXW - 1])
+        nc.scalar.copy(out=rb_sb[:], in_=accs[0][:, FXW : FXW + P])
         dt_ps = bank(0, [P, 2, J], "dt_ps")
         dmax = fin.tile([P, 2], F32, name="dmax", tag="dmax")
         for i in range(2):
-            pieces = [ce_sb[:, i * P : (i + 1) * P], co_sb[:, i * P : (i + 1) * P]]
+            pieces = [ca_sb[:, i * P : (i + 1) * P], cb_sb[:, i * P : (i + 1) * P]]
             if i == 0:
-                pieces.extend([ce_sb[:, N_ROWS:FXW], co_sb[:, N_ROWS:FXW]])
-            pieces.append(rb_sb[:, i * P : (i + 1) * P])
+                pieces.extend([ca_sb[:, N_ROWS:FXW], cb_sb[:, N_ROWS:FXW]])
+            pieces.append(ca_sb[:, FXW : FXW + P] if i == 0 else rb_sb[:])
             for idx, piece in enumerate(pieces):
                 nc.tensor.matmul(
                     out=dt_ps[:, i, :], lhsT=piece, rhs=ident[:], is_transpose=True, start=(idx == 0), stop=(idx == len(pieces) - 1)

@@ -41,7 +41,7 @@ BRIDGE_KICK = 4
 FIRST_KICK = 16
 KICK_EVERY = 16
 KICK = 4
-IDLE_TURNS = 3
+EARLY_KICK = 2
 CAST_SPLIT = 1440
 OUT_W = IN_F + J
 
@@ -251,7 +251,8 @@ def tile_minibatchdiscriminator_kernel(tc, tensor, T, out_0, out_1):
         nc.sync.dma_start(out=hn[:, N_ROWS:FXW], in_=hn[:, 0:WIN])
         nc.sync.dma_start(out=fx[:, 0:LOOPED, N_ROWS:FXW], in_=fx[:, 0:LOOPED, 0:WIN])
 
-        kick(bank(4, [P, 512], "idle"), FIRST_KICK)
+        unread = bank(6, [P, 512], "idle")
+        kick(unread, FIRST_KICK)
 
         sap = ctx.enter_context(tc.tile_pool(name="sap", bufs=3))
         gap = ctx.enter_context(tc.tile_pool(name="gap", bufs=3))
@@ -385,12 +386,11 @@ def tile_minibatchdiscriminator_kernel(tc, tensor, T, out_0, out_1):
                 lbs[g] = bank(4 + g % L_BANKS, [P, R, J], "lb")
                 if g > 0 and g % KICK_EVERY == 0:
                     kick(lbs[g][:].rearrange("p r j -> p (r j)"), KICK)
-            if 0 <= t < 2 * R:
-                for rep in range(IDLE_TURNS):
-                    nc.tensor.transpose(lbs[t // R][:, t % R, :], ident[:], ident[:])
             if 0 <= t < N_ROWS:
                 accumulate_row(t)
-            if t == R:
+            if 0 <= t < 2 * R and t % 2 == 1:
+                kick(unread, EARLY_KICK)
+            if t == 2 * R - 1:
                 for odd in range(2):
                     acc = bank(6 + odd, [P, FXW + P], "acc")
                     accs[1 - odd] = acc

@@ -18,10 +18,9 @@ AX = mybir.AxisListType
 
 P = 128
 R = 4
-S_ROW = (6, 6, 6, 6)
-CHAIN_ROW = (7, 7, 7, 8)
+S_ROW = (7, 6, 7, 6)
+CHAIN_ROW = (7, 8, 7, 8)
 G_ROW = tuple([KD - S_ROW[r] - CHAIN_ROW[r] for r in range(R)])
-G_STARTS = (False, False, False, True)
 S_MAX = max(S_ROW)
 S_MIN = min(S_ROW)
 G_MAX = max(G_ROW)
@@ -30,7 +29,6 @@ PLANES = S_MAX + KD - S_MIN
 LOOPED = S_MAX + KD - min(CHAIN_ROW) - S_MIN
 S_AHEAD = R
 G_AHEAD = 2
-START_AHEAD = C_MAX + 1
 FLT_BIG = 3.0e38
 ONES_W = 24
 GROUPS = N_ROWS // R
@@ -58,6 +56,9 @@ def tile_minibatchdiscriminator_kernel(tc, tensor, T, out_0, out_1):
 
     def gpsimd_ks(m):
         return range(S_ROW[m % R], S_ROW[m % R] + G_ROW[m % R])
+
+    def hn_of(m):
+        return hns[S_ROW[m % R] - S_MIN]
 
     def chain_start(m):
         return C_MAX - CHAIN_ROW[m % R]
@@ -99,7 +100,10 @@ def tile_minibatchdiscriminator_kernel(tc, tensor, T, out_0, out_1):
             fsbi = keep.tile([P, KD, J], F32, name="fsb%d" % i, tag="fsb%d" % i)
             fsb.append(fsbi)
         fx = keep.tile([P, PLANES, FXW], F32, name="fx", tag="fx")
-        hn = keep.tile([P, FXW], F32, name="hn", tag="hn")
+        hns = []
+        for s in range(S_MIN, S_MAX + 1):
+            hns_s = keep.tile([P, FXW], F32, name="hn%d" % s, tag="hn%d" % s)
+            hns.append(hns_s)
         xmax = keep.tile([P, 2], F32, name="xmax", tag="xmax")
         xq = keep.tile([P, 4 * N_ROWS], U32, name="xq", tag="xq", align_bytes=64)
         xs = keep.tile([P, 4 * N_ROWS], U8, name="xs", tag="xs", align_bytes=64)
@@ -209,16 +213,16 @@ def tile_minibatchdiscriminator_kernel(tc, tensor, T, out_0, out_1):
 
         hp = bank(6, [P, N_ROWS], "hp")
         for i in range(2):
-            for k in range(S_MIN, KD):
+            for k in range(S_MAX, KD):
                 nc.tensor.matmul(
                     out=hp[:, i * P : (i + 1) * P],
                     lhsT=fsb[i][:, k, :],
                     rhs=ident[:],
                     is_transpose=True,
-                    start=(k == S_MIN),
+                    start=(k == S_MAX),
                     stop=(k == KD - 1),
                 )
-        nc.vector.tensor_scalar(out=hn[:, 0:N_ROWS], in0=hp[:], scalar1=-0.5, scalar2=None, op0=ALU.mult)
+        nc.vector.tensor_scalar(out=hns[S_MAX - S_MIN][:, 0:N_ROWS], in0=hp[:], scalar1=-0.5, scalar2=None, op0=ALU.mult)
 
         vps = []
         for b in range(C_MAX // 2):
@@ -238,17 +242,22 @@ def tile_minibatchdiscriminator_kernel(tc, tensor, T, out_0, out_1):
                     nc.tensor.transpose(pk[:, kk, i * P : (i + 1) * P], fsb[i][:, k + kk, :], ident[:])
             return pk
 
+        pk = turn_pair(S_MIN, 4)
+        nc.scalar.activation(out=fx[:, S_MIN, 0:N_ROWS], in_=pk[:, 0, :], func=ACT.Copy, scale=0.5)
+        nc.vector.tensor_tensor(
+            out=hns[0][:, 0:N_ROWS], in0=hns[1][:, 0:N_ROWS], in1=fx[:, S_MIN, 0:N_ROWS], op=ALU.subtract
+        )
         for b in range(C_MAX // 2):
             for kk in range(2):
                 turn_chain_plane(2 * b + kk, 0)
             k = chain_k(2 * b)
             nc.vector.tensor_copy(out=fx[:, whole(k) : whole(k) + 2, 0:N_ROWS], in_=vps[b][:])
-            if 2 * b < S_MAX:
-                pk = turn_pair(2 * b, (5, 7, 6)[b])
-                nc.scalar.activation(out=fx[:, 2 * b : 2 * b + 2, 0:N_ROWS], in_=pk[:], func=ACT.Copy, scale=0.5)
-        pk = turn_pair(S_MIN, 7)
+            if 2 * b < S_MIN:
+                spk = turn_pair(2 * b, (5, 7, 6)[b])
+                nc.scalar.activation(out=fx[:, 2 * b : 2 * b + 2, 0:N_ROWS], in_=spk[:], func=ACT.Copy, scale=0.5)
         nc.scalar.copy(out=fx[:, whole(S_MIN) : whole(S_MIN) + 2, 0:N_ROWS], in_=pk[:])
-        nc.sync.dma_start(out=hn[:, N_ROWS:FXW], in_=hn[:, 0:WIN])
+        for hn in hns:
+            nc.sync.dma_start(out=hn[:, N_ROWS:FXW], in_=hn[:, 0:WIN])
         nc.sync.dma_start(out=fx[:, 0:LOOPED, N_ROWS:FXW], in_=fx[:, 0:LOOPED, 0:WIN])
 
         unread = bank(6, [P, 512], "idle")
@@ -293,27 +302,16 @@ def tile_minibatchdiscriminator_kernel(tc, tensor, T, out_0, out_1):
                     op1=ALU.max,
                 )
 
-        def gpsimd_start(m):
-            va = group_tile(vas, vap, m, 1, "va")
-            nc.gpsimd.tensor_scalar(
-                out=va[:, m % R, 0, :],
-                in0=hn[:, m + 1 : m + 1 + WIN],
-                scalar1=1.0,
-                scalar2=hn[:, m : m + 1],
-                op0=ALU.mult,
-                op1=ALU.add,
-            )
-
         def chain_link(m, place):
             chain = group_tile(vas, vap, m, 1, "va")[:, m % R, 0, :]
             k = chain_k(place)
             plane = vps[place // 2][:, place % 2, m % P + 1 : m % P + 1 + WIN]
-            if place == chain_start(m) and not G_STARTS[m % R]:
+            if place == chain_start(m):
                 nc.vector.tensor_scalar(
                     out=chain,
                     in0=plane,
                     scalar1=fx[:, whole(k), m : m + 1],
-                    scalar2=hn[:, m : m + 1],
+                    scalar2=hn_of(m)[:, m : m + 1],
                     op0=ALU.max,
                     op1=ALU.add,
                 )
@@ -333,8 +331,7 @@ def tile_minibatchdiscriminator_kernel(tc, tensor, T, out_0, out_1):
             g, r = divmod(m, R)
             lb = lbs[g]
             srcs = [sas[g][:, r, idx, :] for idx in range(S_ROW[r])]
-            if not G_STARTS[r]:
-                srcs.append(hn[:, m + 1 : m + 1 + WIN])
+            srcs.append(hn_of(m)[:, m + 1 : m + 1 + WIN])
             srcs.extend([gas[g][:, r, idx, :] for idx in range(G_ROW[r])])
             srcs.append(vas[g][:, r, 0, :])
             for idx, src in enumerate(srcs):
@@ -366,11 +363,9 @@ def tile_minibatchdiscriminator_kernel(tc, tensor, T, out_0, out_1):
                 stop=(m == N_ROWS - 1),
             )
 
-        for t in range(-START_AHEAD, N_ROWS + 2 * R):
+        for t in range(-C_MAX, N_ROWS + 2 * R):
             if 0 <= t + S_AHEAD < N_ROWS:
                 scalar_row(t + S_AHEAD)
-            if 0 <= t + START_AHEAD < N_ROWS and G_STARTS[(t + START_AHEAD) % R]:
-                gpsimd_start(t + START_AHEAD)
             if 0 <= t + G_AHEAD < N_ROWS:
                 gpsimd_row(t + G_AHEAD)
             vector_slot(t)

@@ -26,7 +26,6 @@ S_MIN = min(S_ROW)
 G_MAX = max(G_ROW)
 C_MAX = max(CHAIN_ROW)
 PLANES = S_MAX + KD - S_MIN
-LOOPED = S_MAX + KD - min(CHAIN_ROW) - S_MIN
 S_AHEAD = R
 G_AHEAD = 2
 FLT_BIG = 3.0e38
@@ -35,8 +34,12 @@ GROUPS = N_ROWS // R
 WIN = 128
 FXW = N_ROWS + WIN
 L_BANKS = 2
-BRIDGE_KICK = 4
-FIRST_KICK = 16
+PARTS = 3
+FREE_ROWS = (P - 4, P + 8)
+SPLIT_ROWS = 2
+BRIDGE_KICK = 2
+TURN_KICK = 1
+FIRST_KICK = 4
 KICK_EVERY = 16
 KICK = 4
 EARLY_KICK = 2
@@ -136,6 +139,15 @@ def tile_minibatchdiscriminator_kernel(tc, tensor, T, out_0, out_1):
             tq = ph1.tile([P, 4, IN_F], U32, name="tq", tag="tq", align_bytes=64)
             ts = ph1.tile([P, 4, IN_F], U8, name="ts", tag="ts", align_bytes=64)
 
+            tgs = {}
+
+            def interleave(q):
+                tg = ph1.tile([P, 1024, 4], BF16, name="tg", tag="tg", bufs=3, align_bytes=64)
+                tgs[q] = tg
+                raw = raws[q]
+                nc.vector.tensor_copy(out=tg[:, 0:512, :], in_=raw[:, :, 0:512].rearrange("p t w -> p w t"))
+                nc.scalar.copy(out=tg[:, 512:1024, :], in_=raw[:, :, 512:1024].rearrange("p t w -> p w t"))
+
             xg_words = xg[:].bitcast(F32).rearrange("p (g n u) -> p g n u", g=4, u=2)
             for gp in range(2):
                 for i in range(2):
@@ -151,6 +163,7 @@ def tile_minibatchdiscriminator_kernel(tc, tensor, T, out_0, out_1):
                         nc.vector.tensor_copy(out=dst, in_=src)
                     else:
                         nc.scalar.copy(out=dst, in_=src)
+            interleave(0)
             for gp in range(2):
                 nc.vector.quantize_mx(
                     out=xq[:, 512 * gp : 512 * (gp + 1)].bitcast(FP8X4),
@@ -161,15 +174,6 @@ def tile_minibatchdiscriminator_kernel(tc, tensor, T, out_0, out_1):
             for i in range(2):
                 for wq in range(4):
                     fb[(i, wq)] = bank(4 * i + wq, [P, 512], "fb")
-
-            tgs = {}
-
-            def interleave(q):
-                tg = ph1.tile([P, 1024, 4], BF16, name="tg", tag="tg", bufs=3, align_bytes=64)
-                tgs[q] = tg
-                raw = raws[q]
-                nc.vector.tensor_copy(out=tg[:, 0:512, :], in_=raw[:, :, 0:512].rearrange("p t w -> p w t"))
-                nc.scalar.copy(out=tg[:, 512:1024, :], in_=raw[:, :, 512:1024].rearrange("p t w -> p w t"))
 
             def quantise_and_multiply(q, parts):
                 c, h = divmod(q, 2)
@@ -195,11 +199,10 @@ def tile_minibatchdiscriminator_kernel(tc, tensor, T, out_0, out_1):
                                 stop=(c == 3),
                             )
 
-            for q in range(9):
+            for q in range(1, 9):
                 if q < 8:
                     interleave(q)
-                if q >= 1:
-                    quantise_and_multiply(q - 1, 2 if q == 8 else 1)
+                quantise_and_multiply(q - 1, 2 if q == 8 else 1)
 
         for eng, i, wq in (("s", 0, 0), ("s", 0, 1), ("s", 1, 0), ("s", 1, 1), ("v", 0, 2), ("v", 1, 2), ("s", 0, 3), ("v", 1, 3)):
             dst = fsb[i][:, :, 32 * wq : 32 * (wq + 1)]
@@ -211,61 +214,9 @@ def tile_minibatchdiscriminator_kernel(tc, tensor, T, out_0, out_1):
             if (i, wq) == (0, 0):
                 kick(bank(0, [P, 512], "idle"), BRIDGE_KICK)
 
-        hp = bank(6, [P, N_ROWS], "hp")
-        for i in range(2):
-            for k in range(S_MAX, KD):
-                nc.tensor.matmul(
-                    out=hp[:, i * P : (i + 1) * P],
-                    lhsT=fsb[i][:, k, :],
-                    rhs=ident[:],
-                    is_transpose=True,
-                    start=(k == S_MAX),
-                    stop=(k == KD - 1),
-                )
-        nc.vector.tensor_scalar(out=hns[S_MAX - S_MIN][:, 0:N_ROWS], in0=hp[:], scalar1=-0.5, scalar2=None, op0=ALU.mult)
-
-        vps = []
-        for b in range(C_MAX // 2):
-            vps.append(bank(b, [P, 2, N_ROWS], "vp%d" % b))
-
-        def turn_chain_plane(place, first):
-            for half in range(2):
-                i = (first + half) % 2
-                nc.tensor.transpose(
-                    vps[place // 2][:, place % 2, half * P : (half + 1) * P], fsb[i][:, chain_k(place), :], ident[:]
-                )
-
-        def turn_pair(k, b):
-            pk = bank(b, [P, 2, N_ROWS], "pk")
-            for kk in range(2):
-                for i in range(2):
-                    nc.tensor.transpose(pk[:, kk, i * P : (i + 1) * P], fsb[i][:, k + kk, :], ident[:])
-            return pk
-
-        pk = turn_pair(S_MIN, 4)
-        nc.scalar.activation(out=fx[:, S_MIN, 0:N_ROWS], in_=pk[:, 0, :], func=ACT.Copy, scale=0.5)
-        nc.vector.tensor_tensor(
-            out=hns[0][:, 0:N_ROWS], in0=hns[1][:, 0:N_ROWS], in1=fx[:, S_MIN, 0:N_ROWS], op=ALU.subtract
-        )
-        for b in range(C_MAX // 2):
-            for kk in range(2):
-                turn_chain_plane(2 * b + kk, 0)
-            k = chain_k(2 * b)
-            nc.vector.tensor_copy(out=fx[:, whole(k) : whole(k) + 2, 0:N_ROWS], in_=vps[b][:])
-            if 2 * b < S_MIN:
-                spk = turn_pair(2 * b, (5, 7, 6)[b])
-                nc.scalar.activation(out=fx[:, 2 * b : 2 * b + 2, 0:N_ROWS], in_=spk[:], func=ACT.Copy, scale=0.5)
-        nc.scalar.copy(out=fx[:, whole(S_MIN) : whole(S_MIN) + 2, 0:N_ROWS], in_=pk[:])
-        for hn in hns:
-            nc.sync.dma_start(out=hn[:, N_ROWS:FXW], in_=hn[:, 0:WIN])
-        nc.sync.dma_start(out=fx[:, 0:LOOPED, N_ROWS:FXW], in_=fx[:, 0:LOOPED, 0:WIN])
-
-        unread = bank(6, [P, 512], "idle")
-        kick(unread, FIRST_KICK)
-
         sap = ctx.enter_context(tc.tile_pool(name="sap", bufs=3))
         gap = ctx.enter_context(tc.tile_pool(name="gap", bufs=3))
-        vap = ctx.enter_context(tc.tile_pool(name="vap", bufs=5))
+        vap = ctx.enter_context(tc.tile_pool(name="vap", bufs=4))
         epl = ctx.enter_context(tc.tile_pool(name="epl", bufs=3))
         fin = ctx.enter_context(tc.tile_pool(name="fin", bufs=1))
         ca_sb = fin.tile([P, FXW + P], F32, name="ca_sb", tag="ca_sb")
@@ -283,12 +234,80 @@ def tile_minibatchdiscriminator_kernel(tc, tensor, T, out_0, out_1):
                 tiles[g] = made
             return tiles[g]
 
-        def scalar_row(m):
-            sa = group_tile(sas, sap, m, S_MAX, "sa")
-            for idx, k in enumerate(scalar_ks(m)):
-                nc.scalar.activation(
-                    out=sa[:, m % R, idx, :], in_=fx[:, k, m + 1 : m + 1 + WIN], func=ACT.Abs, scale=-1.0, bias=fx[:, k, m : m + 1]
+        unread = bank(7, [P, 512], "idle")
+
+        vps = []
+        for b in range(C_MAX // 2):
+            vps.append(bank(b, [P, 2, N_ROWS], "vp%d" % b))
+
+        def turn_chain_plane(place, first):
+            for half in range(2):
+                i = (first + half) % 2
+                nc.tensor.transpose(
+                    vps[place // 2][:, place % 2, half * P : (half + 1) * P], fsb[i][:, chain_k(place), :], ident[:]
                 )
+
+        def turn_chain_pair(b):
+            for place in (2 * b, 2 * b + 1):
+                turn_chain_plane(place, 0)
+            k = chain_k(2 * b)
+            nc.vector.tensor_copy(out=fx[:, whole(k) : whole(k) + 2, 0:N_ROWS], in_=vps[b][:])
+
+        def turn_pair(k, b):
+            pk = bank(b, [P, 2, N_ROWS], "pk")
+            for kk in range(2):
+                for i in range(2):
+                    nc.tensor.transpose(pk[:, kk, i * P : (i + 1) * P], fsb[i][:, k + kk, :], ident[:])
+            return pk
+
+        def scalar_tile(m, k):
+            sa = group_tile(sas, sap, m, S_MAX, "sa")
+            nc.scalar.activation(
+                out=sa[:, m % R, k, :], in_=fx[:, k, m + 1 : m + 1 + WIN], func=ACT.Abs, scale=-1.0, bias=fx[:, k, m : m + 1]
+            )
+
+        def turn_scalar_pair(k, b):
+            pk = turn_pair(k, b)
+            nc.scalar.activation(out=fx[:, k : k + 2, 0:N_ROWS], in_=pk[:], func=ACT.Copy, scale=0.5)
+            for kk in range(2):
+                scalar_tile(0, k + kk)
+
+        pk = turn_pair(S_MIN, 4)
+        nc.scalar.activation(out=fx[:, S_MIN, 0:N_ROWS], in_=pk[:, 0, :], func=ACT.Copy, scale=0.5)
+        nc.scalar.copy(out=fx[:, whole(S_MIN) : whole(S_MIN) + 2, 0:N_ROWS], in_=pk[:])
+        turn_chain_pair(0)
+        turn_scalar_pair(0, 5)
+        turn_chain_pair(1)
+
+        hp = bank(6, [P, N_ROWS], "hp")
+        for i in range(2):
+            for k in range(S_MAX, KD):
+                nc.tensor.matmul(
+                    out=hp[:, i * P : (i + 1) * P],
+                    lhsT=fsb[i][:, k, :],
+                    rhs=ident[:],
+                    is_transpose=True,
+                    start=(k == S_MAX),
+                    stop=(k == KD - 1),
+                )
+        nc.vector.tensor_scalar(out=hns[S_MAX - S_MIN][:, 0:N_ROWS], in0=hp[:], scalar1=-0.5, scalar2=None, op0=ALU.mult)
+        nc.vector.tensor_tensor(
+            out=hns[0][:, 0:N_ROWS], in0=hns[1][:, 0:N_ROWS], in1=fx[:, S_MIN, 0:N_ROWS], op=ALU.subtract
+        )
+        kick(unread, TURN_KICK)
+        turn_scalar_pair(2, 5)
+        turn_chain_pair(2)
+        turn_scalar_pair(4, 6)
+        turn_chain_pair(3)
+        scalar_tile(0, S_MIN)
+        for hn in hns:
+            nc.sync.dma_start(out=hn[:, N_ROWS:FXW], in_=hn[:, 0:WIN])
+        nc.sync.dma_start(out=fx[:, :, N_ROWS:FXW], in_=fx[:, :, 0:WIN])
+        kick(unread, FIRST_KICK)
+
+        def scalar_row(m):
+            for k in scalar_ks(m):
+                scalar_tile(m, k)
 
         def gpsimd_row(m):
             ga = group_tile(gas, gap, m, G_MAX, "ga")
@@ -302,30 +321,47 @@ def tile_minibatchdiscriminator_kernel(tc, tensor, T, out_0, out_1):
                     op1=ALU.max,
                 )
 
-        def chain_link(m, place):
-            chain = group_tile(vas, vap, m, 1, "va")[:, m % R, 0, :]
+        def chain_link(m, part, place, opens):
+            chain = group_tile(vas, vap, m, PARTS, "va")[:, m % R, part if m < SPLIT_ROWS else 0, :]
             k = chain_k(place)
-            plane = vps[place // 2][:, place % 2, m % P + 1 : m % P + 1 + WIN]
+            if FREE_ROWS[0] <= m < FREE_ROWS[1]:
+                plane = fx[:, whole(k), m + 1 : m + 1 + WIN]
+            else:
+                plane = vps[place // 2][:, place % 2, m % P + 1 : m % P + 1 + WIN]
+            value = fx[:, whole(k), m : m + 1]
             if place == chain_start(m):
                 nc.vector.tensor_scalar(
-                    out=chain,
-                    in0=plane,
-                    scalar1=fx[:, whole(k), m : m + 1],
-                    scalar2=hn_of(m)[:, m : m + 1],
-                    op0=ALU.max,
-                    op1=ALU.add,
+                    out=chain, in0=plane, scalar1=value, scalar2=hn_of(m)[:, m : m + 1], op0=ALU.max, op1=ALU.add
                 )
+            elif opens and m < SPLIT_ROWS:
+                nc.vector.tensor_scalar(out=chain, in0=plane, scalar1=value, scalar2=None, op0=ALU.max)
             else:
-                nc.vector.scalar_tensor_tensor(
-                    out=chain, in0=plane, scalar=fx[:, whole(k), m : m + 1], in1=chain, op0=ALU.max, op1=ALU.add
-                )
+                nc.vector.scalar_tensor_tensor(out=chain, in0=plane, scalar=value, in1=chain, op0=ALU.max, op1=ALU.add)
+
+        def chain_parts(m):
+            places = list(range(chain_start(m), C_MAX))
+            cuts = [(len(places) * part + PARTS - 1) // PARTS for part in range(PARTS + 1)]
+            return [places[cuts[part] : cuts[part + 1]] for part in range(PARTS)]
+
+        def links_of_slot(t):
+            streams = []
+            for part in range(PARTS):
+                m = t if 0 <= t < SPLIT_ROWS else t + PARTS - 1 - part
+                if 0 <= m < N_ROWS and (m >= SPLIT_ROWS or m == t):
+                    streams.append([(m, part, place) for place in chain_parts(m)[part]])
+            if 0 <= t < SPLIT_ROWS:
+                for part in range(PARTS - 1):
+                    m = t + PARTS - 1 - part
+                    if m >= SPLIT_ROWS:
+                        streams.append([(m, part, place) for place in chain_parts(m)[part]])
+            links = []
+            for turn in range(max([len(stream) for stream in streams] + [0])):
+                links.extend([stream[turn] for stream in streams if turn < len(stream)])
+            return links
 
         def vector_slot(t):
-            for d in range(C_MAX):
-                m = t + d
-                place = C_MAX - 1 - d
-                if 0 <= m < N_ROWS and place >= chain_start(m):
-                    chain_link(m, place)
+            for m, part, place in links_of_slot(t):
+                chain_link(m, part, place, place == chain_parts(m)[part][0])
 
         def accumulate_row(m):
             g, r = divmod(m, R)
@@ -333,7 +369,7 @@ def tile_minibatchdiscriminator_kernel(tc, tensor, T, out_0, out_1):
             srcs = [sas[g][:, r, idx, :] for idx in range(S_ROW[r])]
             srcs.append(hn_of(m)[:, m + 1 : m + 1 + WIN])
             srcs.extend([gas[g][:, r, idx, :] for idx in range(G_ROW[r])])
-            srcs.append(vas[g][:, r, 0, :])
+            srcs.extend([vas[g][:, r, part, :] for part in range(PARTS if m < SPLIT_ROWS else 1)])
             for idx, src in enumerate(srcs):
                 nc.tensor.matmul(
                     out=lb[:, r, :], lhsT=src, rhs=ident[:], is_transpose=True, start=(idx == 0), stop=(idx == len(srcs) - 1)
@@ -363,8 +399,8 @@ def tile_minibatchdiscriminator_kernel(tc, tensor, T, out_0, out_1):
                 stop=(m == N_ROWS - 1),
             )
 
-        for t in range(-C_MAX, N_ROWS + 2 * R):
-            if 0 <= t + S_AHEAD < N_ROWS:
+        for t in range(-S_AHEAD, N_ROWS + 2 * R):
+            if 0 < t + S_AHEAD < N_ROWS:
                 scalar_row(t + S_AHEAD)
             if 0 <= t + G_AHEAD < N_ROWS:
                 gpsimd_row(t + G_AHEAD)
@@ -393,8 +429,8 @@ def tile_minibatchdiscriminator_kernel(tc, tensor, T, out_0, out_1):
                         nc.tensor.matmul(
                             out=acc[:, z * P : (z + 1) * P], lhsT=zeros[:], rhs=ident[:], is_transpose=True, start=(z == 0), stop=False
                         )
-            if 0 <= t - (P - C_MAX) < C_MAX:
-                turn_chain_plane(t - (P - C_MAX), 1)
+            if 0 <= t - FREE_ROWS[0] < C_MAX:
+                turn_chain_plane(t - FREE_ROWS[0], 1)
             if 0 <= t - 2 * R < N_ROWS:
                 fold_row(t - 2 * R)
             if t % R == 1 and 0 <= t // R - 1 < GROUPS:

@@ -34,13 +34,13 @@ GROUPS = N_ROWS // R
 WIN = 128
 FXW = N_ROWS + WIN
 L_BANKS = 2
-PARTS = 3
+PARTS = 4
 FREE_ROWS = (P - 4, P + 8)
-SPLIT_ROWS = 2
+SPLIT_ROWS = PARTS - 1
 BRIDGE_KICK = 2
 TURN_KICK = 1
 FIRST_KICK = 4
-KICK_EVERY = 16
+KICK_EVERY = 32
 KICK = 4
 EARLY_KICK = 2
 CAST_SPLIT = 1440

@@ -18,29 +18,31 @@ AX = mybir.AxisListType
 
 P = 128
 R = 4
-S_ROW = (7, 6, 7, 6)
-CHAIN_ROW = (7, 8, 7, 8)
+S_ROW = (7, 6, 6, 6)
+CHAIN_ROW = (7, 8, 7, 7)
 G_ROW = tuple([KD - S_ROW[r] - CHAIN_ROW[r] for r in range(R)])
+G_STARTS = (False, False, False, True)
 S_MAX = max(S_ROW)
 S_MIN = min(S_ROW)
 G_MAX = max(G_ROW)
 C_MAX = max(CHAIN_ROW)
 PLANES = S_MAX + KD - S_MIN
+PARTS = 4
 S_AHEAD = R
 G_AHEAD = 2
+START_AHEAD = PARTS + 4
 FLT_BIG = 3.0e38
 ONES_W = 24
 GROUPS = N_ROWS // R
 WIN = 128
 FXW = N_ROWS + WIN
 L_BANKS = 2
-PARTS = 4
 FREE_ROWS = (P - 4, P + 8)
 SPLIT_ROWS = PARTS - 1
-BRIDGE_KICK = 2
-TURN_KICK = 1
-FIRST_KICK = 4
-KICK_EVERY = 32
+BRIDGE_KICK = 4
+TURN_KICK = 2
+FIRST_KICK = 6
+KICK_EVERY = 16
 KICK = 4
 EARLY_KICK = 2
 CAST_SPLIT = 1440
@@ -81,9 +83,10 @@ def tile_minibatchdiscriminator_kernel(tc, tensor, T, out_0, out_1):
         make_identity(nc, ident[:])
         zeros = keep.tile([P, P], F32, name="zeros", tag="zeros")
         nc.vector.memset(zeros[:], 0.0)
+        ones_at = ONES_W - 1
         ones = keep.tile([P, 2 * ONES_W], F32, name="ones", tag="ones")
         nc.vector.memset(ones[:], 0.0)
-        nc.vector.memset(ones[:, ONES_W - 1 : ONES_W], 1.0)
+        nc.vector.memset(ones[:, ones_at : ones_at + 1], 1.0)
         warm = keep.tile([P, 1], F32, name="warm", tag="warm")
         nc.scalar.activation(out=warm[:], in_=zeros[:, 0:1], func=ACT.Exp)
         maskb = keep.tile([P, 1], F32, name="maskb", tag="maskb")
@@ -216,7 +219,7 @@ def tile_minibatchdiscriminator_kernel(tc, tensor, T, out_0, out_1):
 
         sap = ctx.enter_context(tc.tile_pool(name="sap", bufs=3))
         gap = ctx.enter_context(tc.tile_pool(name="gap", bufs=3))
-        vap = ctx.enter_context(tc.tile_pool(name="vap", bufs=4))
+        vap = ctx.enter_context(tc.tile_pool(name="vap", bufs=5))
         epl = ctx.enter_context(tc.tile_pool(name="epl", bufs=3))
         fin = ctx.enter_context(tc.tile_pool(name="fin", bufs=1))
         ca_sb = fin.tile([P, FXW + P], F32, name="ca_sb", tag="ca_sb")
@@ -321,6 +324,19 @@ def tile_minibatchdiscriminator_kernel(tc, tensor, T, out_0, out_1):
                     op1=ALU.max,
                 )
 
+        def gpsimd_starts(m):
+            return G_STARTS[m % R] and m >= SPLIT_ROWS
+
+        def gpsimd_start(m):
+            nc.gpsimd.tensor_scalar(
+                out=group_tile(vas, vap, m, PARTS, "va")[:, m % R, 0, :],
+                in0=hn_of(m)[:, m + 1 : m + 1 + WIN],
+                scalar1=1.0,
+                scalar2=hn_of(m)[:, m : m + 1],
+                op0=ALU.mult,
+                op1=ALU.add,
+            )
+
         def chain_link(m, part, place, opens):
             chain = group_tile(vas, vap, m, PARTS, "va")[:, m % R, part if m < SPLIT_ROWS else 0, :]
             k = chain_k(place)
@@ -329,7 +345,7 @@ def tile_minibatchdiscriminator_kernel(tc, tensor, T, out_0, out_1):
             else:
                 plane = vps[place // 2][:, place % 2, m % P + 1 : m % P + 1 + WIN]
             value = fx[:, whole(k), m : m + 1]
-            if place == chain_start(m):
+            if place == chain_start(m) and not gpsimd_starts(m):
                 nc.vector.tensor_scalar(
                     out=chain, in0=plane, scalar1=value, scalar2=hn_of(m)[:, m : m + 1], op0=ALU.max, op1=ALU.add
                 )
@@ -367,7 +383,8 @@ def tile_minibatchdiscriminator_kernel(tc, tensor, T, out_0, out_1):
             g, r = divmod(m, R)
             lb = lbs[g]
             srcs = [sas[g][:, r, idx, :] for idx in range(S_ROW[r])]
-            srcs.append(hn_of(m)[:, m + 1 : m + 1 + WIN])
+            if not gpsimd_starts(m):
+                srcs.append(hn_of(m)[:, m + 1 : m + 1 + WIN])
             srcs.extend([gas[g][:, r, idx, :] for idx in range(G_ROW[r])])
             srcs.extend([vas[g][:, r, part, :] for part in range(PARTS if m < SPLIT_ROWS else 1)])
             for idx, src in enumerate(srcs):
@@ -390,7 +407,7 @@ def tile_minibatchdiscriminator_kernel(tc, tensor, T, out_0, out_1):
             )
             half, col = divmod(m, P)
             left = min(col - col % 2, P - ONES_W)
-            skip = ONES_W - 1 - (col - left)
+            skip = ones_at - (col - left)
             nc.tensor.matmul(
                 out=accs[1 - half][:, FXW + left : FXW + left + ONES_W],
                 lhsT=ets[g][:, r, :],
@@ -399,9 +416,11 @@ def tile_minibatchdiscriminator_kernel(tc, tensor, T, out_0, out_1):
                 stop=(m == N_ROWS - 1),
             )
 
-        for t in range(-S_AHEAD, N_ROWS + 2 * R):
+        for t in range(-max(S_AHEAD, START_AHEAD), N_ROWS + 2 * R):
             if 0 < t + S_AHEAD < N_ROWS:
                 scalar_row(t + S_AHEAD)
+            if 0 <= t + START_AHEAD < N_ROWS and gpsimd_starts(t + START_AHEAD):
+                gpsimd_start(t + START_AHEAD)
             if 0 <= t + G_AHEAD < N_ROWS:
                 gpsimd_row(t + G_AHEAD)
             vector_slot(t)

@@ -37,12 +37,12 @@ GROUPS = N_ROWS // R
 WIN = 128
 FXW = N_ROWS + WIN
 L_BANKS = 2
-FREE_ROWS = (P - 4, P + 8)
+FREE_ROWS = (P - 2, P)
 SPLIT_ROWS = PARTS - 1
-BRIDGE_KICK = 4
-TURN_KICK = 2
+BRIDGE_KICK = 6
+TURN_KICK = 1
 FIRST_KICK = 6
-KICK_EVERY = 16
+KICK_GROUPS = (4, 32)
 KICK = 4
 EARLY_KICK = 2
 CAST_SPLIT = 1440
@@ -431,10 +431,13 @@ def tile_minibatchdiscriminator_kernel(tc, tensor, T, out_0, out_1):
                     )
                 nc.vector.reciprocal(out=xrcp[:], in_=xmax[:])
                 nc.vector.tensor_scalar(out=xfac[:], in0=xrcp[:], scalar1=448.0, scalar2=None, op0=ALU.mult)
+                for i in range(2):
+                    nc.vector.tensor_copy(out=o32[i][:, 0:IN_F], in_=xb[i][:])
+                    nc.sync.dma_start(out=out_0[i * P : (i + 1) * P, 0:IN_F], in_=o32[i][:, 0:IN_F])
             if 0 <= t < N_ROWS and t % R == 0:
                 g = t // R
                 lbs[g] = bank(4 + g % L_BANKS, [P, R, J], "lb")
-                if g > 0 and g % KICK_EVERY == 0:
+                if g in KICK_GROUPS:
                     kick(lbs[g][:].rearrange("p r j -> p (r j)"), KICK)
             if 0 <= t < N_ROWS:
                 accumulate_row(t)
@@ -448,16 +451,13 @@ def tile_minibatchdiscriminator_kernel(tc, tensor, T, out_0, out_1):
                         nc.tensor.matmul(
                             out=acc[:, z * P : (z + 1) * P], lhsT=zeros[:], rhs=ident[:], is_transpose=True, start=(z == 0), stop=False
                         )
-            if 0 <= t - FREE_ROWS[0] < C_MAX:
-                turn_chain_plane(t - FREE_ROWS[0], 1)
+            for place in range(C_MAX):
+                if t == FREE_ROWS[0] - PARTS + 1 + place * PARTS // C_MAX:
+                    turn_chain_plane(place, 1)
             if 0 <= t - 2 * R < N_ROWS:
                 fold_row(t - 2 * R)
             if t % R == 1 and 0 <= t // R - 1 < GROUPS:
                 expo(t // R - 1)
-            if t == N_ROWS - 1:
-                for i in range(2):
-                    nc.scalar.copy(out=o32[i][:, 0:IN_F], in_=xb[i][:])
-                    nc.sync.dma_start(out=out_0[i * P : (i + 1) * P, 0:IN_F], in_=o32[i][:, 0:IN_F])
 
         nc.vector.tensor_copy(out=ca_sb[:], in_=accs[1][:])
         nc.scalar.copy(out=cb_sb[:, 1:FXW], in_=accs[0][:, 0 : FXW - 1])

from contextlib import ExitStack

import concourse.mybir as mybir
from concourse.masks import make_identity

N_ROWS, IN_F, J, KD = 256, 2048, 128, 16
FLOPS = 2 * N_ROWS * IN_F * J * KD + 3 * N_ROWS * N_ROWS * J * KD

F32 = mybir.dt.float32
BF16 = mybir.dt.bfloat16
U32 = mybir.dt.uint32
U8 = mybir.dt.uint8
FP8X4 = mybir.dt.float8_e4m3fn_x4
FP8 = mybir.dt.float8_e4m3fn
ALU = mybir.AluOpType
ACT = mybir.ActivationFunctionType
AX = mybir.AxisListType

P = 128
R = 4
S_ROW = (7, 6, 6, 6)
CHAIN_ROW = (7, 8, 7, 7)
G_ROW = tuple([KD - S_ROW[r] - CHAIN_ROW[r] for r in range(R)])
G_STARTS = (False, False, False, True)
S_MAX = max(S_ROW)
S_MIN = min(S_ROW)
G_MAX = max(G_ROW)
C_MAX = max(CHAIN_ROW)
PLANES = S_MAX + KD - S_MIN
PARTS = 4
S_AHEAD = R
G_AHEAD = 2
START_AHEAD = PARTS + 4
FLT_BIG = 3.0e38
ONES_W = 24
GROUPS = N_ROWS // R
WIN = 128
FXW = N_ROWS + WIN
L_BANKS = 2
FREE_ROWS = (P - 2, P)
SPLIT_ROWS = PARTS - 1
BRIDGE_KICK = 6
TURN_KICK = 1
FIRST_KICK = 6
KICK_GROUPS = (4, 32)
KICK = 4
EARLY_KICK = 2
CAST_SPLIT = 1440
OUT_W = IN_F + J


def tile_minibatchdiscriminator_kernel(tc, tensor, T, out_0, out_1):
    nc = tc.nc
    t_mat = T.rearrange("i j k -> i (j k)")

    def whole(k):
        return S_MAX + k - S_MIN

    def scalar_ks(m):
        return range(S_ROW[m % R])

    def gpsimd_ks(m):
        return range(S_ROW[m % R], S_ROW[m % R] + G_ROW[m % R])

    def hn_of(m):
        return hns[S_ROW[m % R] - S_MIN]

    def chain_start(m):
        return C_MAX - CHAIN_ROW[m % R]

    def chain_k(place):
        return KD - C_MAX + place

    with ExitStack() as ctx:
        ctx.enter_context(tc.manual_schedule())
        keep = ctx.enter_context(tc.tile_pool(name="keep", bufs=1))
        psum = ctx.enter_context(tc.psum_pool(name="psum", bufs=1))

        def bank(b, shape, name):
            return psum.tile(shape, F32, name=name, tag="bank%d" % b)

        ident = keep.tile([P, P], F32, name="ident", tag="ident")
        make_identity(nc, ident[:])
        zeros = keep.tile([P, P], F32, name="zeros", tag="zeros")
        nc.vector.memset(zeros[:], 0.0)
        ones_at = ONES_W - 1
        ones = keep.tile([P, 2 * ONES_W], F32, name="ones", tag="ones")
        nc.vector.memset(ones[:], 0.0)
        nc.vector.memset(ones[:, ones_at : ones_at + 1], 1.0)
        warm = keep.tile([P, 1], F32, name="warm", tag="warm")
        nc.scalar.activation(out=warm[:], in_=zeros[:, 0:1], func=ACT.Exp)
        maskb = keep.tile([P, 1], F32, name="maskb", tag="maskb")
        nc.vector.tensor_scalar(out=maskb[:], in0=ident[:, P - 1 : P], scalar1=-30000.0, scalar2=None, op0=ALU.mult)

        xb = []
        for i in range(2):
            xbi = keep.tile([P, IN_F], BF16, name="xb%d" % i, tag="xb%d" % i)
            nc.sync.dma_start(out=xbi[:], in_=tensor[i * P : (i + 1) * P, :])
            xb.append(xbi)
        o32 = []
        for i in range(2):
            o32i = keep.tile([P, OUT_W], F32, name="o32_%d" % i, tag="o32_%d" % i)
            o32.append(o32i)
        fsb = []
        for i in range(2):
            fsbi = keep.tile([P, KD, J], F32, name="fsb%d" % i, tag="fsb%d" % i)
            fsb.append(fsbi)
        fx = keep.tile([P, PLANES, FXW], F32, name="fx", tag="fx")
        hns = []
        for s in range(S_MIN, S_MAX + 1):
            hns_s = keep.tile([P, FXW], F32, name="hn%d" % s, tag="hn%d" % s)
            hns.append(hns_s)
        xmax = keep.tile([P, 2], F32, name="xmax", tag="xmax")
        xq = keep.tile([P, 4 * N_ROWS], U32, name="xq", tag="xq", align_bytes=64)
        xs = keep.tile([P, 4 * N_ROWS], U8, name="xs", tag="xs", align_bytes=64)

        def kick(unread, passes):
            for rep in range(passes):
                nc.tensor.matmul_mx(
                    out=unread[:],
                    lhsT=xq[:, 0:P].bitcast(FP8X4),
                    lhsT_scale=xs[:, 0:P],
                    rhs=xq[:, 0:512].bitcast(FP8X4),
                    rhs_scale=xs[:, 0:512],
                    start=True,
                    stop=True,
                )

        fb = {}
        with tc.tile_pool(name="ph1", bufs=1) as ph1:
            raws = []
            for q in range(8):
                c, h = divmod(q, 2)
                raw = ph1.tile([P, 4, 1024], BF16, name="raw", tag="raw", bufs=8)
                nc.sync.dma_start(
                    out=raw[:],
                    in_=t_mat[512 * c : 512 * (c + 1), 1024 * h : 1024 * (h + 1)].rearrange("(p t) w -> p t w", t=4),
                )
                raws.append(raw)

            xg = ph1.tile([P, 4 * N_ROWS * 4], BF16, name="xg", tag="xg", align_bytes=64)
            tq = ph1.tile([P, 4, IN_F], U32, name="tq", tag="tq", align_bytes=64)
            ts = ph1.tile([P, 4, IN_F], U8, name="ts", tag="ts", align_bytes=64)

            tgs = {}

            def interleave(q):
                tg = ph1.tile([P, 1024, 4], BF16, name="tg", tag="tg", bufs=3, align_bytes=64)
                tgs[q] = tg
                raw = raws[q]
                nc.vector.tensor_copy(out=tg[:, 0:512, :], in_=raw[:, :, 0:512].rearrange("p t w -> p w t"))
                nc.scalar.copy(out=tg[:, 512:1024, :], in_=raw[:, :, 512:1024].rearrange("p t w -> p w t"))

            xg_words = xg[:].bitcast(F32).rearrange("p (g n u) -> p g n u", g=4, u=2)
            for gp in range(2):
                for i in range(2):
                    words = xb[i][:].bitcast(F32)
                    xt = bank(2 * gp + i, [P, 2, 2, P], "xt")
                    for gg in range(2):
                        g = 2 * gp + gg
                        for u in range(2):
                            nc.tensor.transpose(xt[:, gg, u, :], words[:, 256 * g + u : 256 * (g + 1) : 2], ident[:])
                    dst = xg_words[:, 2 * gp : 2 * gp + 2, i * P : (i + 1) * P, :]
                    src = xt[:].rearrange("p g u r -> p g r u")
                    if i == 0:
                        nc.vector.tensor_copy(out=dst, in_=src)
                    else:
                        nc.scalar.copy(out=dst, in_=src)
            interleave(0)
            for gp in range(2):
                nc.vector.quantize_mx(
                    out=xq[:, 512 * gp : 512 * (gp + 1)].bitcast(FP8X4),
                    scales=xs[:, 512 * gp : 512 * (gp + 1)],
                    in_=xg[:, 2048 * gp : 2048 * (gp + 1)],
                )

            for i in range(2):
                for wq in range(4):
                    fb[(i, wq)] = bank(4 * i + wq, [P, 512], "fb")

            def quantise_and_multiply(q, parts):
                c, h = divmod(q, 2)
                width = 1024 // parts
                for part in range(parts):
                    first = 1024 * h + width * part
                    nc.vector.quantize_mx(
                        out=tq[:, c, first : first + width].bitcast(FP8X4),
                        scales=ts[:, c, first : first + width],
                        in_=tgs[q][:, width * part : width * (part + 1), :].rearrange("p w t -> p (w t)"),
                    )
                    for wq in range(first // 512, (first + width) // 512):
                        for i in range(2):
                            n_cols = slice(256 * c + P * i, 256 * c + P * (i + 1))
                            w_cols = slice(512 * wq, 512 * (wq + 1))
                            nc.tensor.matmul_mx(
                                out=fb[(i, wq)][:],
                                lhsT=xq[:, n_cols].bitcast(FP8X4),
                                lhsT_scale=xs[:, n_cols],
                                rhs=tq[:, c, w_cols].bitcast(FP8X4),
                                rhs_scale=ts[:, c, w_cols],
                                start=(c == 0),
                                stop=(c == 3),
                            )

            for q in range(1, 9):
                if q < 8:
                    interleave(q)
                quantise_and_multiply(q - 1, 2 if q == 8 else 1)

        for eng, i, wq in (("s", 0, 0), ("s", 0, 1), ("s", 1, 0), ("s", 1, 1), ("v", 0, 2), ("v", 1, 2), ("s", 0, 3), ("v", 1, 3)):
            dst = fsb[i][:, :, 32 * wq : 32 * (wq + 1)]
            src = fb[(i, wq)][:].rearrange("p (j k) -> p k j", k=KD)
            if eng == "v":
                nc.vector.tensor_copy(out=dst, in_=src)
            else:
                nc.scalar.copy(out=dst, in_=src)
            if (i, wq) == (0, 0):
                kick(bank(0, [P, 512], "idle"), BRIDGE_KICK)

        sap = ctx.enter_context(tc.tile_pool(name="sap", bufs=3))
        gap = ctx.enter_context(tc.tile_pool(name="gap", bufs=3))
        vap = ctx.enter_context(tc.tile_pool(name="vap", bufs=5))
        epl = ctx.enter_context(tc.tile_pool(name="epl", bufs=3))
        fin = ctx.enter_context(tc.tile_pool(name="fin", bufs=1))
        ca_sb = fin.tile([P, FXW + P], F32, name="ca_sb", tag="ca_sb")
        cb_sb = fin.tile([P, FXW], F32, name="cb_sb", tag="cb_sb")
        rb_sb = fin.tile([P, P], F32, name="rb_sb", tag="rb_sb")
        xrcp = fin.tile([P, 2], F32, name="xrcp", tag="xrcp")
        xfac = fin.tile([P, 2], F32, name="xfac", tag="xfac")
        nc.vector.memset(cb_sb[:, 0:1], 0.0)
        sas, gas, vas, lbs, ets, accs = {}, {}, {}, {}, {}, {}

        def group_tile(tiles, pool, m, count, name):
            g = m // R
            if g not in tiles:
                made = pool.tile([P, R, count, WIN], F32, name=name, tag=name)
                tiles[g] = made
            return tiles[g]

        unread = bank(7, [P, 512], "idle")

        vps = []
        for b in range(C_MAX // 2):
            vps.append(bank(b, [P, 2, N_ROWS], "vp%d" % b))

        def turn_chain_plane(place, first):
            for half in range(2):
                i = (first + half) % 2
                nc.tensor.transpose(
                    vps[place // 2][:, place % 2, half * P : (half + 1) * P], fsb[i][:, chain_k(place), :], ident[:]
                )

        def turn_chain_pair(b):
            for place in (2 * b, 2 * b + 1):
                turn_chain_plane(place, 0)
            k = chain_k(2 * b)
            nc.vector.tensor_copy(out=fx[:, whole(k) : whole(k) + 2, 0:N_ROWS], in_=vps[b][:])

        def turn_pair(k, b):
            pk = bank(b, [P, 2, N_ROWS], "pk")
            for kk in range(2):
                for i in range(2):
                    nc.tensor.transpose(pk[:, kk, i * P : (i + 1) * P], fsb[i][:, k + kk, :], ident[:])
            return pk

        def scalar_tile(m, k):
            sa = group_tile(sas, sap, m, S_MAX, "sa")
            nc.scalar.activation(
                out=sa[:, m % R, k, :], in_=fx[:, k, m + 1 : m + 1 + WIN], func=ACT.Abs, scale=-1.0, bias=fx[:, k, m : m + 1]
            )

        def turn_scalar_pair(k, b):
            pk = turn_pair(k, b)
            nc.scalar.activation(out=fx[:, k : k + 2, 0:N_ROWS], in_=pk[:], func=ACT.Copy, scale=0.5)
            for kk in range(2):
                scalar_tile(0, k + kk)

        pk = turn_pair(S_MIN, 4)
        nc.scalar.activation(out=fx[:, S_MIN, 0:N_ROWS], in_=pk[:, 0, :], func=ACT.Copy, scale=0.5)
        nc.scalar.copy(out=fx[:, whole(S_MIN) : whole(S_MIN) + 2, 0:N_ROWS], in_=pk[:])
        turn_chain_pair(0)
        turn_scalar_pair(0, 5)
        turn_chain_pair(1)

        hp = bank(6, [P, N_ROWS], "hp")
        for i in range(2):
            for k in range(S_MAX, KD):
                nc.tensor.matmul(
                    out=hp[:, i * P : (i + 1) * P],
                    lhsT=fsb[i][:, k, :],
                    rhs=ident[:],
                    is_transpose=True,
                    start=(k == S_MAX),
                    stop=(k == KD - 1),
                )
        nc.vector.tensor_scalar(out=hns[S_MAX - S_MIN][:, 0:N_ROWS], in0=hp[:], scalar1=-0.5, scalar2=None, op0=ALU.mult)
        nc.vector.tensor_tensor(
            out=hns[0][:, 0:N_ROWS], in0=hns[1][:, 0:N_ROWS], in1=fx[:, S_MIN, 0:N_ROWS], op=ALU.subtract
        )
        kick(unread, TURN_KICK)
        turn_scalar_pair(2, 5)
        turn_chain_pair(2)
        turn_scalar_pair(4, 6)
        turn_chain_pair(3)
        scalar_tile(0, S_MIN)
        for hn in hns:
            nc.sync.dma_start(out=hn[:, N_ROWS:FXW], in_=hn[:, 0:WIN])
        nc.sync.dma_start(out=fx[:, :, N_ROWS:FXW], in_=fx[:, :, 0:WIN])
        kick(unread, FIRST_KICK)

        def scalar_row(m):
            for k in scalar_ks(m):
                scalar_tile(m, k)

        def gpsimd_row(m):
            ga = group_tile(gas, gap, m, G_MAX, "ga")
            for idx, k in enumerate(gpsimd_ks(m)):
                nc.gpsimd.tensor_scalar(
                    out=ga[:, m % R, idx, :],
                    in0=fx[:, whole(k), m + 1 : m + 1 + WIN],
                    scalar1=FLT_BIG,
                    scalar2=fx[:, whole(k), m : m + 1],
                    op0=ALU.min,
                    op1=ALU.max,
                )

        def gpsimd_starts(m):
            return G_STARTS[m % R] and m >= SPLIT_ROWS

        def gpsimd_start(m):
            nc.gpsimd.tensor_scalar(
                out=group_tile(vas, vap, m, PARTS, "va")[:, m % R, 0, :],
                in0=hn_of(m)[:, m + 1 : m + 1 + WIN],
                scalar1=1.0,
                scalar2=hn_of(m)[:, m : m + 1],
                op0=ALU.mult,
                op1=ALU.add,
            )

        def chain_link(m, part, place, opens):
            chain = group_tile(vas, vap, m, PARTS, "va")[:, m % R, part if m < SPLIT_ROWS else 0, :]
            k = chain_k(place)
            if FREE_ROWS[0] <= m < FREE_ROWS[1]:
                plane = fx[:, whole(k), m + 1 : m + 1 + WIN]
            else:
                plane = vps[place // 2][:, place % 2, m % P + 1 : m % P + 1 + WIN]
            value = fx[:, whole(k), m : m + 1]
            if place == chain_start(m) and not gpsimd_starts(m):
                nc.vector.tensor_scalar(
                    out=chain, in0=plane, scalar1=value, scalar2=hn_of(m)[:, m : m + 1], op0=ALU.max, op1=ALU.add
                )
            elif opens and m < SPLIT_ROWS:
                nc.vector.tensor_scalar(out=chain, in0=plane, scalar1=value, scalar2=None, op0=ALU.max)
            else:
                nc.vector.scalar_tensor_tensor(out=chain, in0=plane, scalar=value, in1=chain, op0=ALU.max, op1=ALU.add)

        def chain_parts(m):
            places = list(range(chain_start(m), C_MAX))
            cuts = [(len(places) * part + PARTS - 1) // PARTS for part in range(PARTS + 1)]
            return [places[cuts[part] : cuts[part + 1]] for part in range(PARTS)]

        def links_of_slot(t):
            streams = []
            for part in range(PARTS):
                m = t if 0 <= t < SPLIT_ROWS else t + PARTS - 1 - part
                if 0 <= m < N_ROWS and (m >= SPLIT_ROWS or m == t):
                    streams.append([(m, part, place) for place in chain_parts(m)[part]])
            if 0 <= t < SPLIT_ROWS:
                for part in range(PARTS - 1):
                    m = t + PARTS - 1 - part
                    if m >= SPLIT_ROWS:
                        streams.append([(m, part, place) for place in chain_parts(m)[part]])
            links = []
            for turn in range(max([len(stream) for stream in streams] + [0])):
                links.extend([stream[turn] for stream in streams if turn < len(stream)])
            return links

        def vector_slot(t):
            for m, part, place in links_of_slot(t):
                chain_link(m, part, place, place == chain_parts(m)[part][0])

        def accumulate_row(m):
            g, r = divmod(m, R)
            lb = lbs[g]
            srcs = [sas[g][:, r, idx, :] for idx in range(S_ROW[r])]
            if not gpsimd_starts(m):
                srcs.append(hn_of(m)[:, m + 1 : m + 1 + WIN])
            srcs.extend([gas[g][:, r, idx, :] for idx in range(G_ROW[r])])
            srcs.extend([vas[g][:, r, part, :] for part in range(PARTS if m < SPLIT_ROWS else 1)])
            for idx, src in enumerate(srcs):
                nc.tensor.matmul(
                    out=lb[:, r, :], lhsT=src, rhs=ident[:], is_transpose=True, start=(idx == 0), stop=(idx == len(srcs) - 1)
                )

        def expo(g):
            et = epl.tile([P, R, J], F32, name="et", tag="et")
            ets[g] = et
            bias = maskb[:, 0:1] if R * g >= WIN else zeros[:, 0:1]
            nc.scalar.activation(out=et[:], in_=lbs[g][:], func=ACT.Exp, scale=-2.0, bias=bias)

        def fold_row(m):
            g, r = divmod(m, R)
            odd = m % 2
            first = m + 1 if odd else m
            nc.tensor.matmul(
                out=accs[odd][:, first : first + WIN], lhsT=ets[g][:, r, :], rhs=ident[:], is_transpose=True, start=False, stop=(m == N_ROWS - 1)
            )
            half, col = divmod(m, P)
            left = min(col - col % 2, P - ONES_W)
            skip = ones_at - (col - left)
            nc.tensor.matmul(
                out=accs[1 - half][:, FXW + left : FXW + left + ONES_W],
                lhsT=ets[g][:, r, :],
                rhs=ones[:, skip : skip + ONES_W],
                start=False,
                stop=(m == N_ROWS - 1),
            )

        for t in range(-max(S_AHEAD, START_AHEAD), N_ROWS + 2 * R):
            if 0 < t + S_AHEAD < N_ROWS:
                scalar_row(t + S_AHEAD)
            if 0 <= t + START_AHEAD < N_ROWS and gpsimd_starts(t + START_AHEAD):
                gpsimd_start(t + START_AHEAD)
            if 0 <= t + G_AHEAD < N_ROWS:
                gpsimd_row(t + G_AHEAD)
            vector_slot(t)
            if t == N_ROWS:
                for i in range(2):
                    nc.vector.tensor_reduce(
                        out=xmax[:, i : i + 1], in_=xb[i][:], axis=AX.X, op=ALU.max, apply_absolute_value=True
                    )
                nc.vector.reciprocal(out=xrcp[:], in_=xmax[:])
                nc.vector.tensor_scalar(out=xfac[:], in0=xrcp[:], scalar1=448.0, scalar2=None, op0=ALU.mult)
                for i in range(2):
                    nc.vector.tensor_copy(out=o32[i][:, 0:IN_F], in_=xb[i][:])
                    nc.sync.dma_start(out=out_0[i * P : (i + 1) * P, 0:IN_F], in_=o32[i][:, 0:IN_F])
            if 0 <= t < N_ROWS and t % R == 0:
                g = t // R
                lbs[g] = bank(4 + g % L_BANKS, [P, R, J], "lb")
                if g in KICK_GROUPS:
                    kick(lbs[g][:].rearrange("p r j -> p (r j)"), KICK)
            if 0 <= t < N_ROWS:
                accumulate_row(t)
            if 0 <= t < 2 * R and t % 2 == 1:
                kick(unread, EARLY_KICK)
            if t == 2 * R - 1:
                for odd in range(2):
                    acc = bank(6 + odd, [P, FXW + P], "acc")
                    accs[1 - odd] = acc
                    for z in range(R):
                        nc.tensor.matmul(
                            out=acc[:, z * P : (z + 1) * P], lhsT=zeros[:], rhs=ident[:], is_transpose=True, start=(z == 0), stop=False
                        )
            for place in range(C_MAX):
                if t == FREE_ROWS[0] - PARTS + 1 + place * PARTS // C_MAX:
                    turn_chain_plane(place, 1)
            if 0 <= t - 2 * R < N_ROWS:
                fold_row(t - 2 * R)
            if t % R == 1 and 0 <= t // R - 1 < GROUPS:
                expo(t // R - 1)

        nc.vector.tensor_copy(out=ca_sb[:], in_=accs[1][:])
        nc.scalar.copy(out=cb_sb[:, 1:FXW], in_=accs[0][:, 0 : FXW - 1])
        nc.scalar.copy(out=rb_sb[:], in_=accs[0][:, FXW : FXW + P])
        dt_ps = bank(0, [P, 2, J], "dt_ps")
        dmax = fin.tile([P, 2], F32, name="dmax", tag="dmax")
        for i in range(2):
            pieces = [ca_sb[:, i * P : (i + 1) * P], cb_sb[:, i * P : (i + 1) * P]]
            if i == 0:
                pieces.extend([ca_sb[:, N_ROWS:FXW], cb_sb[:, N_ROWS:FXW]])
            pieces.append(ca_sb[:, FXW : FXW + P] if i == 0 else rb_sb[:])
            for idx, piece in enumerate(pieces):
                nc.tensor.matmul(
                    out=dt_ps[:, i, :], lhsT=piece, rhs=ident[:], is_transpose=True, start=(idx == 0), stop=(idx == len(pieces) - 1)
                )
        for i in range(2):
            nc.vector.tensor_scalar(
                out=o32[i][:, IN_F:OUT_W],
                in0=dt_ps[:, i, :],
                scalar1=1.0,
                scalar2=None,
                op0=ALU.add,
                op1=ALU.max,
                accum_out=dmax[:, i : i + 1],
            )
            nc.sync.dma_start(out=out_0[i * P : (i + 1) * P, IN_F:OUT_W], in_=o32[i][:, IN_F:OUT_W])
        rcp = fin.tile([P, 2], F32, name="rcp", tag="rcp")
        nc.vector.reciprocal(out=rcp[:], in_=dmax[:])
        fac = fin.tile([P, 2], F32, name="fac", tag="fac")
        nc.vector.scalar_tensor_tensor(out=fac[:], in0=rcp[:], scalar=448.0, in1=xfac[:], op0=ALU.mult, op1=ALU.min)
        for i in range(2):
            rows = slice(i * P, (i + 1) * P)
            o8v = fin.tile([P, CAST_SPLIT], FP8, name="o8v%d" % i, tag="o8v%d" % i)
            o8s = fin.tile([P, OUT_W - CAST_SPLIT], FP8, name="o8s%d" % i, tag="o8s%d" % i)
            nc.vector.tensor_scalar(
                out=o8v[:], in0=o32[i][:, 0:CAST_SPLIT], scalar1=fac[:, i : i + 1], scalar2=None, op0=ALU.mult, saturate=False
            )
            nc.scalar.activation(
                out=o8s[:],
                in_=o32[i][:, CAST_SPLIT:OUT_W],
                func=ACT.Identity,
                scale=fac[:, i : i + 1],
                bias=zeros[:, 0:1],
                saturate=False,
            )
            nc.sync.dma_start(out=out_1[rows, 0:CAST_SPLIT], in_=o8v[:].bitcast(U8))
            nc.sync.dma_start(out=out_1[rows, CAST_SPLIT:OUT_W], in_=o8s[:].bitcast(U8))
